import numpy as np
import ml_dtypes


def mxq(x, axis, fmt="e4m3"):
    dtype, down = {"e4m3": (ml_dtypes.float8_e4m3fn, 7), "e5m2": (ml_dtypes.float8_e5m2, 14)}[fmt]
    v = np.moveaxis(np.asarray(x, np.float32).astype(ml_dtypes.bfloat16).astype(np.float64), axis, -1)
    blocks = v.reshape(v.shape[:-1] + (-1, 32))
    amax = np.abs(blocks).max(-1, keepdims=True)
    byte = np.maximum(np.where(amax > 0, np.frexp(amax)[1] - 1 + 127, 0) - down, 1)
    scale = np.exp2(byte - 127.0)
    codes = (blocks / scale).astype(np.float32).astype(dtype).astype(np.float64)
    return np.moveaxis((codes * scale).reshape(v.shape), -1, axis)


WIDE = False


def mx_kscale(k):
    if not WIDE:
        return np.ones(k)
    levels = np.array([10, -10, 5, -5, 0])
    a = np.random.permutation(np.resize(levels, k // 512 * 4)).reshape(k // 512, 4)
    idx = np.arange(k)
    return np.exp2(a[idx // 512, idx % 128 // 32])


BF16 = ml_dtypes.bfloat16


def bf(x):
    return np.asarray(x, np.float32).astype(BF16)


def f64(x):
    return np.asarray(x).astype(np.float64)


N, NFEAT, NHID, NOUT, NCLS = 1024, 512, 512, 512, 128
C = NHID + NHID + NOUT
SPAN = 60.0
LAM = SPAN * np.log(2.0)


def log_softmax(v):
    v = v - v.max(axis=1, keepdims=True)
    return v - np.log(np.exp(v).sum(axis=1, keepdims=True))


def setup_inputs():
    t = mx_kscale(C)
    t1, t2, t3 = t[:NHID], t[NHID:NHID + NHID], t[NHID + NHID:]
    return {
        "x1": bf(np.maximum(np.random.standard_normal((N, NHID)), 0.0) * 0.75 * t1),
        "x2": bf(np.maximum(np.random.standard_normal((N, NHID)), 0.0) * t2),
        "adj": bf(np.exp2(-SPAN * np.random.uniform(size=(N, N))) * (LAM / N)),
        "W3": bf(np.random.standard_normal((NHID, NOUT)) * (1.4 / np.sqrt(NHID)) / t2[:, None] * t3),
        "b3": bf(np.random.standard_normal(NOUT) * 0.3 * t3),
        "Wl": bf(np.random.standard_normal((C, NCLS)) * (3.0 / np.sqrt(C)) / t[:, None]),
        "bl": bf(np.random.standard_normal(NCLS) * 0.3),
    }


def reference(x1, x2, adj, W3, b3, Wl, bl):
    support = f64(x2) @ f64(W3)
    x3 = (mxq(f64(adj), 1, "e4m3") @ mxq(support, 0, "e4m3")) + f64(b3)
    cat = np.concatenate((f64(x1), f64(x2), x3), axis=1)
    logits = (mxq(cat, 1, "e4m3") @ mxq(f64(Wl), 0, "e4m3")) + f64(bl)
    return log_softmax(logits)

@@ -1,0 +1,367 @@
+from contextlib import ExitStack
+
+import concourse.mybir as mybir
+from concourse.masks import make_identity
+
+F32 = mybir.dt.float32
+BF16 = mybir.dt.bfloat16
+U32 = mybir.dt.uint32
+U8 = mybir.dt.uint8
+FP8X4 = mybir.dt.float8_e4m3fn_x4
+ACT = mybir.ActivationFunctionType
+ALU = mybir.AluOpType
+AX = mybir.AxisListType
+
+P = 128
+FLOPS = 2 * 1024 * 512 * 512 + 2 * 1024 * 1024 * 512 + 2 * 1024 * 1536 * 128
+
+N_T_BANKS = 5
+WEAVE = ((), (2, 3), (4, 5), (6, 7), (8, 9), (10, 11), (12, 13), (14, 15))
+V_EVAC = (0, 3, 5, 7)
+S_PATH = (1, 3)
+X_BANK = (7, 5, 6, 1, 2, 3, 7, 5)
+L_BANK = (4, 0)
+PINNED = True
+
+
+def tile_gcn_pb_kernel(tc, x1, x2, adj, W3, b3, Wl, bl, out):
+    nc = tc.nc
+    with ExitStack() as ctx:
+        keep = ctx.enter_context(tc.tile_pool(name="keep", bufs=1))
+        work = ctx.enter_context(tc.tile_pool(name="work", bufs=2))
+        psum = ctx.enter_context(tc.psum_pool(name="psum", bufs=1))
+        if PINNED:
+            ctx.enter_context(tc.manual_schedule())
+
+        def bank(n, shape, name):
+            return psum.tile(shape, F32, tag="bank%d" % n, name=name)
+
+        def node_view(x):
+            return x.rearrange("(s m e) k -> m s e k", s=4, m=P, e=2)
+
+        def load_nodes(dst, src, s0, ns):
+            nc.sync.dma_start(
+                out=dst[:, 2 * s0 : 2 * (s0 + ns), :].rearrange("p (s e) k -> p s e k", e=2),
+                in_=node_view(src)[:, s0 : s0 + ns],
+            )
+
+        ident = keep.tile([P, P], F32, name="ident")
+        make_identity(nc, ident[:])
+        zrows = keep.tile([P, P], BF16, name="zrows")
+        nc.vector.memset(zrows[:], 0.0)
+        ident_bf = keep.tile([P, P], BF16, name="ident_bf")
+        nc.vector.tensor_copy(out=ident_bf[:], in_=ident[:])
+        nc.scalar.dma_start(out=zrows[0:4, :], in_=b3.rearrange("(r c) -> r c", r=4))
+        nc.scalar.dma_start(out=zrows[4:5, :], in_=bl.rearrange("(r c) -> r c", r=1))
+
+        x2_sb = keep.tile([P, 8, 512], BF16, name="x2_sb")
+        x1_sb = keep.tile([P, 8, 512], BF16, name="x1_sb")
+        adj_sb = keep.tile([P, 8, 1024], BF16, name="adj_sb")
+        w3_sb = keep.tile([P, 4, 512], BF16, name="w3_sb")
+        wl_sb = keep.tile([P, 12, P], BF16, name="wl_sb")
+        load_nodes(x2_sb, x2, 0, 2)
+        nc.sync.dma_start(
+            out=w3_sb[:].rearrange("p (u e) c -> p u e c", e=2),
+            in_=W3.rearrange("(u q e) c -> q u e c", u=2, q=P, e=2),
+        )
+        load_nodes(x2_sb, x2, 2, 2)
+        for s in range(4):
+            load_nodes(adj_sb, adj, s, 1)
+        load_nodes(x1_sb, x1, 0, 2)
+        load_nodes(x1_sb, x1, 2, 2)
+        nc.sync.dma_start(
+            out=wl_sb[:, 0:8, :].rearrange("p (cu e) n -> p cu e n", e=2),
+            in_=Wl[0:1024, :].rearrange("(cu q e) n -> q cu e n", cu=4, q=P, e=2),
+        )
+        nc.sync.dma_start(
+            out=wl_sb[:, 8:12, :], in_=Wl[1024:1536, :].rearrange("(t p) n -> p t n", t=4, p=P)
+        )
+
+        x2w = x2_sb[:].bitcast(F32)
+        x1w = x1_sb[:].bitcast(F32)
+        adjw = adj_sb[:].bitcast(F32)
+
+        tps = {}
+        grouped = {}
+        codes = {}
+        scales = {}
+
+        def t_in(k, j):
+            if k < 4:
+                return x2w[:, 2 * k + j // 2, P * (j % 2) : P * (j % 2) + P]
+            if k < 12:
+                return adjw[:, k - 4, P * j : P * j + P]
+            return x1w[:, 2 * (k - 12) + j // 2, P * (j % 2) : P * (j % 2) + P]
+
+        def transpose(k, j):
+            if j == 0:
+                tps[k] = bank(k % N_T_BANKS, [P, 4, P], "tp%d" % k)
+            nc.tensor.transpose(tps[k][:, j, :], t_in(k, j), ident[:])
+
+        def evac_t(k):
+            grouped[k] = keep.tile([P, 2, P, 4], BF16, name="grouped%d" % k, align_bytes=64)
+            o = grouped[k][:].bitcast(F32)
+            i = tps[k][:].rearrange("p (a u) m -> p a m u", a=2)
+            if k in V_EVAC:
+                nc.vector.tensor_copy(out=o, in_=i)
+            else:
+                nc.scalar.copy(out=o, in_=i)
+
+        def quant_t(k):
+            codes[k] = keep.tile([P, 256], U32, name="codes%d" % k, align_bytes=64)
+            scales[k] = keep.tile([P, 256], U8, name="scales%d" % k, align_bytes=64)
+            nc.vector.quantize_mx(
+                out=codes[k][:].bitcast(FP8X4),
+                scales=scales[k][:],
+                in_=grouped[k][:].rearrange("p a m t -> p (a m t)"),
+            )
+
+        for k in (0, 1):
+            for j in range(4):
+                transpose(k, j)
+        cps = bank(7, [P, 2, P], "cps")
+        nc.tensor.matmul(out=cps[:, 0, :], lhsT=zrows[:], rhs=ident_bf[:], start=True, stop=True)
+        nc.tensor.matmul(
+            out=cps[:, 1, :], lhsT=ident_bf[:, 4:5].to_broadcast([P, P]), rhs=zrows[:], start=True, stop=True
+        )
+        evac_t(0)
+        evac_t(1)
+        consts = keep.tile([P, 2, P], F32, name="consts")
+        nc.vector.tensor_copy(out=consts[:], in_=cps[:])
+        quant_t(0)
+        quant_t(1)
+
+        planes = [keep.tile([P, 4, 512], BF16, name="planes%d" % g) for g in range(2)]
+        gs = [keep.tile([P, 512, 4], BF16, name="gs%d" % g, align_bytes=64) for g in range(2)]
+        cs = [keep.tile([P, 512], U32, name="cs%d" % g, align_bytes=64) for g in range(2)]
+        ss = [keep.tile([P, 512], U8, name="ss%d" % g, align_bytes=64) for g in range(2)]
+
+        def regroup_s(g, f0, nf):
+            nc.vector.tensor_copy(
+                out=gs[g][:, f0 : f0 + nf, :].rearrange("p (c i) t -> p c t i", i=4),
+                in_=planes[g][:, :, f0 : f0 + nf].rearrange("p t (c i) -> p c t i", i=4),
+            )
+
+        def quant_s(g, f0, nf):
+            nc.vector.quantize_mx(
+                out=cs[g][:, f0 : f0 + nf].bitcast(FP8X4),
+                scales=ss[g][:, f0 : f0 + nf],
+                in_=gs[g][:, f0 : f0 + nf, :].rearrange("p f t -> p (f t)"),
+            )
+
+        for i in range(8):
+            acc = bank(5 + i % 3, [P, 512], "acc%d" % i)
+            w = WEAVE[i]
+            for tk in range(4):
+                nc.tensor.matmul(
+                    out=acc[:],
+                    lhsT=grouped[i // 2][:, i % 2, :, tk],
+                    rhs=w3_sb[:, tk, :],
+                    start=(tk == 0),
+                    stop=(tk == 3),
+                )
+                if w:
+                    transpose(w[tk // 2], 2 * (tk % 2))
+                    transpose(w[tk // 2], 2 * (tk % 2) + 1)
+            early = w and w[0] < 12
+            if early:
+                evac_t(w[0])
+            if i < 7:
+                nc.scalar.copy(out=planes[i // 4][:, i % 4, :], in_=acc[:])
+            else:
+                for c in range(4):
+                    nc.scalar.copy(
+                        out=planes[1][:, 3, P * c : P * c + P], in_=acc[:, P * c : P * c + P]
+                    )
+            if early:
+                evac_t(w[1])
+                quant_t(w[0])
+            if i == 3:
+                regroup_s(0, 0, 512)
+                quant_s(0, 0, 512)
+            if early:
+                quant_t(w[1])
+
+        regroup_s(1, 0, P)
+        regroup_s(1, P, P)
+        quant_s(1, 0, P)
+        regroup_s(1, 2 * P, P)
+        quant_s(1, P, P)
+        regroup_s(1, 3 * P, P)
+        quant_s(1, 2 * P, P)
+        quant_s(1, 3 * P, P)
+
+        gw = keep.tile([P, 3, P, 4], BF16, name="gw", align_bytes=64)
+        cw = keep.tile([P, 3, P], U32, name="cw", align_bytes=64)
+        sw = keep.tile([P, 3, P], U8, name="sw", align_bytes=64)
+        for c in range(3):
+            nc.scalar.copy(
+                out=gw[:, c].rearrange("p (c i) t -> p c t i", i=4),
+                in_=wl_sb[:, 4 * c : 4 * c + 4, :].rearrange("p t (c i) -> p c t i", i=4),
+            )
+        for c in range(3):
+            nc.vector.quantize_mx(
+                out=cw[:, c, :].bitcast(FP8X4),
+                scales=sw[:, c, :],
+                in_=gw[:, c].rearrange("p n t -> p (n t)"),
+            )
+        for k in (12, 13, 14, 15):
+            evac_t(k)
+
+        z = keep.tile([P, 8, P], F32, name="z")
+        res = keep.tile([P, 8, P], F32, name="res")
+        negmax = keep.tile([P, 8], F32, name="negmax")
+        sums = keep.tile([P, 8], F32, name="sums")
+        x3ps = {}
+        gx3 = {}
+        c3 = {}
+        s3 = {}
+        l3 = {}
+
+        def x_pass(a, tf):
+            if tf == 0:
+                x3ps[a] = bank(X_BANK[a], [P, 4, P], "x3ps%d" % a)
+            fs = slice(P * tf, P * tf + P)
+            for g in range(2):
+                nc.tensor.matmul_mx(
+                    out=x3ps[a][:, tf, :],
+                    lhsT=cs[g][:, fs].bitcast(FP8X4),
+                    lhsT_scale=ss[g][:, fs],
+                    rhs=codes[4 + a][:, P * g : P * g + P].bitcast(FP8X4),
+                    rhs_scale=scales[4 + a][:, P * g : P * g + P],
+                    start=(g == 0),
+                    stop=(g == 1),
+                )
+
+        def x_evac_scalar(a):
+            pl = work.tile([P, 4, P], BF16, tag="x3pl", name="x3pl%d" % a)
+            for tf in range(4):
+                nc.scalar.activation(
+                    out=pl[:, tf, :],
+                    in_=x3ps[a][:, tf, :],
+                    func=ACT.Identity,
+                    bias=consts[:, 0, tf : tf + 1],
+                    scale=1.0,
+                )
+            return pl
+
+        def x_regroup(a, pl):
+            gx3[a] = keep.tile([P, P, 4], BF16, name="gx3_%d" % a, align_bytes=64)
+            nc.vector.tensor_copy(
+                out=gx3[a][:].rearrange("p (c i) t -> p c t i", i=4),
+                in_=pl[:].rearrange("p t (c i) -> p c t i", i=4),
+            )
+
+        def x_evac_vector(a):
+            gx3[a] = keep.tile([P, P, 4], BF16, name="gx3_%d" % a, align_bytes=64)
+            nc.vector.tensor_tensor(
+                out=gx3[a][:],
+                in0=x3ps[a][:].rearrange("p t m -> p m t"),
+                in1=consts[:, 0, 0:4].unsqueeze(1).to_broadcast([P, P, 4]),
+                op=ALU.add,
+            )
+
+        def x_quant(a):
+            c3[a] = keep.tile([P, P], U32, name="c3_%d" % a, align_bytes=64)
+            s3[a] = keep.tile([P, P], U8, name="s3_%d" % a, align_bytes=64)
+            nc.vector.quantize_mx(
+                out=c3[a][:].bitcast(FP8X4), scales=s3[a][:], in_=gx3[a][:].rearrange("p m t -> p (m t)")
+            )
+
+        def logits(a):
+            l3[a] = bank(L_BANK[a % 2], [P, P], "l3_%d" % a)
+            cols = slice(P * (a % 2), P * (a % 2) + P)
+            parts = (
+                (codes[12 + a // 2][:, cols], scales[12 + a // 2][:, cols]),
+                (codes[a // 2][:, cols], scales[a // 2][:, cols]),
+                (c3[a][:], s3[a][:]),
+            )
+            for c in range(3):
+                nc.tensor.matmul_mx(
+                    out=l3[a][:],
+                    lhsT=parts[c][0].bitcast(FP8X4),
+                    lhsT_scale=parts[c][1],
+                    rhs=cw[:, c, :].bitcast(FP8X4),
+                    rhs_scale=sw[:, c, :],
+                    start=(c == 0),
+                    stop=(c == 2),
+                )
+
+        def z_max(a):
+            nc.vector.tensor_tensor(out=z[:, a, :], in0=l3[a][:], in1=consts[:, 1, :], op=ALU.add)
+            nc.vector.tensor_reduce(
+                out=negmax[:, a : a + 1], in_=z[:, a, :], axis=AX.X, op=ALU.max, negate=True
+            )
+
+        def exp_sum(a):
+            junk = work.tile([P, P], BF16, tag="junk", name="junk%d" % a)
+            nc.scalar.activation(
+                out=junk[:],
+                in_=z[:, a, :],
+                func=ACT.Exp,
+                bias=negmax[:, a : a + 1],
+                scale=1.0,
+                accum_out=sums[:, a : a + 1],
+            )
+
+        for tf in range(4):
+            for a in range(4):
+                x_pass(a, tf)
+        quant_t(12)
+        quant_t(13)
+        x_evac_vector(0)
+        pl1 = x_evac_scalar(1)
+        pl3 = x_evac_scalar(3)
+        x_quant(0)
+        quant_t(14)
+        quant_t(15)
+        x_evac_vector(2)
+        for tf in range(4):
+            x_pass(4, tf)
+        logits(0)
+        z_max(0)
+        exp_sum(0)
+        x_regroup(1, pl1)
+        x_quant(1)
+        x_quant(2)
+        x_regroup(3, pl3)
+        x_quant(3)
+        logits(1)
+        logits(2)
+        z_max(1)
+        exp_sum(1)
+        z_max(2)
+        exp_sum(2)
+        for a in range(4, 8):
+            if a < 7:
+                for tf in range(4):
+                    x_pass(a + 1, tf)
+            logits(a - 1)
+            x_evac_vector(a)
+            z_max(a - 1)
+            exp_sum(a - 1)
+            x_quant(a)
+        logits(7)
+        z_max(7)
+        exp_sum(7)
+
+        logs = keep.tile([P, 8], F32, name="logs")
+        nc.scalar.activation(out=logs[:], in_=sums[:], func=ACT.Ln)
+        shift = keep.tile([P, 8], F32, name="shift")
+        nc.vector.tensor_tensor(out=shift[:], in0=negmax[:], in1=logs[:], op=ALU.subtract)
+        out_v = out.rearrange("(s m e) c -> m s e c", s=4, m=P, e=2)
+        for a in range(8):
+            if a % 2 == 0:
+                nc.vector.tensor_scalar(
+                    out=res[:, a, :], in0=z[:, a, :], scalar1=shift[:, a : a + 1], scalar2=None, op0=ALU.add
+                )
+            else:
+                nc.scalar.activation(
+                    out=res[:, a, :], in_=z[:, a, :], func=ACT.Identity, bias=shift[:, a : a + 1], scale=1.0
+                )
+            if a % 4 == 3:
+                h = a // 4
+                nc.sync.dma_start(
+                    out=out_v[:, 2 * h : 2 * h + 2],
+                    in_=res[:, 4 * h : 4 * h + 4, :].rearrange("p (s e) c -> p s e c", e=2),
+                )

@@ -21,7 +21,7 @@ V_EVAC = (0, 3, 5, 7)
 S_PATH = (1, 3)
 X_BANK = (7, 5, 6, 1, 2, 3, 7, 5)
 L_BANK = (4, 0)
-PINNED = True
+PINNED = False
 
 
 def tile_gcn_pb_kernel(tc, x1, x2, adj, W3, b3, Wl, bl, out):

@@ -16,12 +16,9 @@ P = 128
 FLOPS = 2 * 1024 * 512 * 512 + 2 * 1024 * 1024 * 512 + 2 * 1024 * 1536 * 128
 
 N_T_BANKS = 5
-WEAVE = ((), (2, 3), (4, 5), (6, 7), (8, 9), (10, 11), (12, 13), (14, 15))
-V_EVAC = (0, 3, 5, 7)
-S_PATH = (1, 3)
-X_BANK = (7, 5, 6, 1, 2, 3, 7, 5)
-L_BANK = (4, 0)
-PINNED = False
+V_EVAC = (0, 3, 5, 7, 13, 14)
+X_BANK = ((7, 5, 1, 6), (2, 3, 4, 0))
+L_BANK = (7, 5, 1, 6)
 
 
 def tile_gcn_pb_kernel(tc, x1, x2, adj, W3, b3, Wl, bl, out):
@@ -30,8 +27,7 @@ def tile_gcn_pb_kernel(tc, x1, x2, adj, W3, b3, Wl, bl, out):
         keep = ctx.enter_context(tc.tile_pool(name="keep", bufs=1))
         work = ctx.enter_context(tc.tile_pool(name="work", bufs=2))
         psum = ctx.enter_context(tc.psum_pool(name="psum", bufs=1))
-        if PINNED:
-            ctx.enter_context(tc.manual_schedule())
+        ctx.enter_context(tc.manual_schedule())
 
         def bank(n, shape, name):
             return psum.tile(shape, F32, tag="bank%d" % n, name=name)
@@ -59,16 +55,13 @@ def tile_gcn_pb_kernel(tc, x1, x2, adj, W3, b3, Wl, bl, out):
         adj_sb = keep.tile([P, 8, 1024], BF16, name="adj_sb")
         w3_sb = keep.tile([P, 4, 512], BF16, name="w3_sb")
         wl_sb = keep.tile([P, 12, P], BF16, name="wl_sb")
-        load_nodes(x2_sb, x2, 0, 2)
+        load_nodes(x2_sb, x2, 0, 1)
         nc.sync.dma_start(
             out=w3_sb[:].rearrange("p (u e) c -> p u e c", e=2),
             in_=W3.rearrange("(u q e) c -> q u e c", u=2, q=P, e=2),
         )
+        load_nodes(x2_sb, x2, 1, 1)
         load_nodes(x2_sb, x2, 2, 2)
-        for s in range(4):
-            load_nodes(adj_sb, adj, s, 1)
-        load_nodes(x1_sb, x1, 0, 2)
-        load_nodes(x1_sb, x1, 2, 2)
         nc.sync.dma_start(
             out=wl_sb[:, 0:8, :].rearrange("p (cu e) n -> p cu e n", e=2),
             in_=Wl[0:1024, :].rearrange("(cu q e) n -> q cu e n", cu=4, q=P, e=2),
@@ -76,6 +69,10 @@ def tile_gcn_pb_kernel(tc, x1, x2, adj, W3, b3, Wl, bl, out):
         nc.sync.dma_start(
             out=wl_sb[:, 8:12, :], in_=Wl[1024:1536, :].rearrange("(t p) n -> p t n", t=4, p=P)
         )
+        for s in range(4):
+            load_nodes(adj_sb, adj, s, 1)
+        load_nodes(x1_sb, x1, 0, 2)
+        load_nodes(x1_sb, x1, 2, 2)
 
         x2w = x2_sb[:].bitcast(F32)
         x1w = x1_sb[:].bitcast(F32)
@@ -83,15 +80,21 @@ def tile_gcn_pb_kernel(tc, x1, x2, adj, W3, b3, Wl, bl, out):
 
         tps = {}
         grouped = {}
-        codes = {}
-        scales = {}
+        cx2 = keep.tile([P, 1024], U32, name="cx2", align_bytes=64)
+        sx2 = keep.tile([P, 1024], U8, name="sx2", align_bytes=64)
+        cx1 = keep.tile([P, 1024], U32, name="cx1", align_bytes=64)
+        sx1 = keep.tile([P, 1024], U8, name="sx1", align_bytes=64)
+        ca = [keep.tile([P, 1024], U32, name="ca%d" % g, align_bytes=64) for g in range(2)]
+        sa = [keep.tile([P, 1024], U8, name="sa%d" % g, align_bytes=64) for g in range(2)]
 
         def t_in(k, j):
+            a2, u = j // 2, j % 2
             if k < 4:
-                return x2w[:, 2 * k + j // 2, P * (j % 2) : P * (j % 2) + P]
+                return x2w[:, 2 * k + a2, P * u : P * u + P]
             if k < 12:
-                return adjw[:, k - 4, P * j : P * j + P]
-            return x1w[:, 2 * (k - 12) + j // 2, P * (j % 2) : P * (j % 2) + P]
+                s, g = (k - 4) // 2, (k - 4) % 2
+                return adjw[:, 2 * s + a2, 256 * g + P * u : 256 * g + P * u + P]
+            return x1w[:, 2 * (k - 12) + a2, P * u : P * u + P]
 
         def transpose(k, j):
             if j == 0:
@@ -108,39 +111,34 @@ def tile_gcn_pb_kernel(tc, x1, x2, adj, W3, b3, Wl, bl, out):
                 nc.scalar.copy(out=o, in_=i)
 
         def quant_t(k):
-            codes[k] = keep.tile([P, 256], U32, name="codes%d" % k, align_bytes=64)
-            scales[k] = keep.tile([P, 256], U8, name="scales%d" % k, align_bytes=64)
+            if k < 4:
+                c, s, q = cx2, sx2, k
+            elif k < 12:
+                c, s, q = ca[(k - 4) % 2], sa[(k - 4) % 2], (k - 4) // 2
+            else:
+                c, s, q = cx1, sx1, k - 12
             nc.vector.quantize_mx(
-                out=codes[k][:].bitcast(FP8X4),
-                scales=scales[k][:],
+                out=c[:, 256 * q : 256 * q + 256].bitcast(FP8X4),
+                scales=s[:, 256 * q : 256 * q + 256],
                 in_=grouped[k][:].rearrange("p a m t -> p (a m t)"),
             )
-
-        for k in (0, 1):
-            for j in range(4):
-                transpose(k, j)
-        cps = bank(7, [P, 2, P], "cps")
-        nc.tensor.matmul(out=cps[:, 0, :], lhsT=zrows[:], rhs=ident_bf[:], start=True, stop=True)
-        nc.tensor.matmul(
-            out=cps[:, 1, :], lhsT=ident_bf[:, 4:5].to_broadcast([P, P]), rhs=zrows[:], start=True, stop=True
-        )
-        evac_t(0)
-        evac_t(1)
-        consts = keep.tile([P, 2, P], F32, name="consts")
-        nc.vector.tensor_copy(out=consts[:], in_=cps[:])
-        quant_t(0)
-        quant_t(1)
 
         planes = [keep.tile([P, 4, 512], BF16, name="planes%d" % g) for g in range(2)]
         gs = [keep.tile([P, 512, 4], BF16, name="gs%d" % g, align_bytes=64) for g in range(2)]
         cs = [keep.tile([P, 512], U32, name="cs%d" % g, align_bytes=64) for g in range(2)]
         ss = [keep.tile([P, 512], U8, name="ss%d" % g, align_bytes=64) for g in range(2)]
+        accs = {}
 
-        def regroup_s(g, f0, nf):
-            nc.vector.tensor_copy(
-                out=gs[g][:, f0 : f0 + nf, :].rearrange("p (c i) t -> p c t i", i=4),
-                in_=planes[g][:, :, f0 : f0 + nf].rearrange("p t (c i) -> p c t i", i=4),
-            )
+        def regroup(eng, dst, src):
+            o = dst.rearrange("p (c i) t -> p c t i", i=4)
+            i = src.rearrange("p t (c i) -> p c t i", i=4)
+            if eng == "v":
+                nc.vector.tensor_copy(out=o, in_=i)
+            else:
+                nc.scalar.copy(out=o, in_=i)
+
+        def regroup_s(eng, g, f0, nf):
+            regroup(eng, gs[g][:, f0 : f0 + nf, :], planes[g][:, :, f0 : f0 + nf])
 
         def quant_s(g, f0, nf):
             nc.vector.quantize_mx(
@@ -149,133 +147,180 @@ def tile_gcn_pb_kernel(tc, x1, x2, adj, W3, b3, Wl, bl, out):
                 in_=gs[g][:, f0 : f0 + nf, :].rearrange("p f t -> p (f t)"),
             )
 
-        for i in range(8):
-            acc = bank(5 + i % 3, [P, 512], "acc%d" % i)
-            w = WEAVE[i]
+        def support_matmuls(i):
+            accs[i] = bank(5 + i % 3, [P, 512], "acc%d" % i)
             for tk in range(4):
                 nc.tensor.matmul(
-                    out=acc[:],
+                    out=accs[i][:],
                     lhsT=grouped[i // 2][:, i % 2, :, tk],
                     rhs=w3_sb[:, tk, :],
                     start=(tk == 0),
                     stop=(tk == 3),
                 )
-                if w:
-                    transpose(w[tk // 2], 2 * (tk % 2))
-                    transpose(w[tk // 2], 2 * (tk % 2) + 1)
-            early = w and w[0] < 12
-            if early:
-                evac_t(w[0])
+                if i > 0:
+                    k = 2 * i + tk // 2
+                    transpose(k, 2 * (tk % 2))
+                    transpose(k, 2 * (tk % 2) + 1)
+
+        def evac_s(i):
             if i < 7:
-                nc.scalar.copy(out=planes[i // 4][:, i % 4, :], in_=acc[:])
+                nc.scalar.copy(out=planes[i // 4][:, i % 4, :], in_=accs[i][:])
             else:
                 for c in range(4):
                     nc.scalar.copy(
-                        out=planes[1][:, 3, P * c : P * c + P], in_=acc[:, P * c : P * c + P]
+                        out=planes[1][:, 3, P * c : P * c + P], in_=accs[i][:, P * c : P * c + P]
                     )
-            if early:
-                evac_t(w[1])
-                quant_t(w[0])
-            if i == 3:
-                regroup_s(0, 0, 512)
-                quant_s(0, 0, 512)
-            if early:
-                quant_t(w[1])
-
-        regroup_s(1, 0, P)
-        regroup_s(1, P, P)
-        quant_s(1, 0, P)
-        regroup_s(1, 2 * P, P)
-        quant_s(1, P, P)
-        regroup_s(1, 3 * P, P)
-        quant_s(1, 2 * P, P)
-        quant_s(1, 3 * P, P)
 
         gw = keep.tile([P, 3, P, 4], BF16, name="gw", align_bytes=64)
         cw = keep.tile([P, 3, P], U32, name="cw", align_bytes=64)
         sw = keep.tile([P, 3, P], U8, name="sw", align_bytes=64)
-        for c in range(3):
-            nc.scalar.copy(
-                out=gw[:, c].rearrange("p (c i) t -> p c t i", i=4),
-                in_=wl_sb[:, 4 * c : 4 * c + 4, :].rearrange("p t (c i) -> p c t i", i=4),
-            )
-        for c in range(3):
-            nc.vector.quantize_mx(
-                out=cw[:, c, :].bitcast(FP8X4),
-                scales=sw[:, c, :],
-                in_=gw[:, c].rearrange("p n t -> p (n t)"),
-            )
-        for k in (12, 13, 14, 15):
-            evac_t(k)
+
+        def wl_quant():
+            for c in range(3):
+                regroup("v", gw[:, c], wl_sb[:, 4 * c : 4 * c + 4, :])
+            for c in range(3):
+                nc.vector.quantize_mx(
+                    out=cw[:, c, :].bitcast(FP8X4),
+                    scales=sw[:, c, :],
+                    in_=gw[:, c].rearrange("p n t -> p (n t)"),
+                )
+
+        for j in range(4):
+            transpose(0, j)
+        cps = bank(7, [P, 2, P], "cps")
+        nc.tensor.matmul(out=cps[:, 0, :], lhsT=zrows[:], rhs=ident_bf[:], start=True, stop=True)
+        nc.tensor.matmul(
+            out=cps[:, 1, :], lhsT=ident_bf[:, 4:5].to_broadcast([P, P]), rhs=zrows[:], start=True, stop=True
+        )
+        for j in range(4):
+            transpose(1, j)
+        evac_t(0)
+        evac_t(1)
+        consts = keep.tile([P, 2, P], F32, name="consts")
+        nc.vector.tensor_copy(out=consts[:], in_=cps[:])
+
+        support_matmuls(0)
+        evac_s(0)
+        quant_t(0)
+        quant_t(1)
+        wl_quant()
+
+        support_matmuls(1)
+        evac_t(2)
+        evac_s(1)
+        evac_t(3)
+
+        support_matmuls(2)
+        evac_t(4)
+        evac_s(2)
+        evac_t(5)
+        quant_t(4)
+
+        support_matmuls(3)
+        evac_t(6)
+        evac_s(3)
+        evac_t(7)
+        quant_t(5)
+        quant_t(6)
+
+        support_matmuls(4)
+        evac_t(8)
+        evac_s(4)
+        evac_t(9)
+        regroup_s("v", 0, 0, 512)
+        quant_s(0, 0, 512)
+        quant_t(7)
+
+        support_matmuls(5)
+        evac_t(10)
+        evac_s(5)
+        evac_t(11)
+        quant_t(8)
+        quant_t(9)
+        quant_t(2)
+
+        support_matmuls(6)
+        evac_t(12)
+        evac_s(6)
+        quant_t(10)
+        quant_t(11)
+        evac_t(13)
+        quant_t(3)
+
+        support_matmuls(7)
+        evac_s(7)
+        regroup_s("s", 1, P, P)
+        regroup_s("s", 1, 3 * P, P)
+        evac_t(15)
+        evac_t(14)
+        regroup_s("v", 1, 0, P)
+        quant_s(1, 0, P)
+        regroup_s("v", 1, 2 * P, P)
+        quant_s(1, P, P)
+        quant_s(1, 2 * P, P)
+        quant_s(1, 3 * P, P)
 
         z = keep.tile([P, 8, P], F32, name="z")
         res = keep.tile([P, 8, P], F32, name="res")
         negmax = keep.tile([P, 8], F32, name="negmax")
         sums = keep.tile([P, 8], F32, name="sums")
+        pl3 = [keep.tile([P, 4, 512], BF16, name="pl3_%d" % h) for h in range(2)]
+        gx3 = [keep.tile([P, 512, 4], BF16, name="gx3_%d" % h, align_bytes=64) for h in range(2)]
+        c3 = [keep.tile([P, 512], U32, name="c3_%d" % h, align_bytes=64) for h in range(2)]
+        s3 = [keep.tile([P, 512], U8, name="s3_%d" % h, align_bytes=64) for h in range(2)]
         x3ps = {}
-        gx3 = {}
-        c3 = {}
-        s3 = {}
         l3 = {}
 
-        def x_pass(a, tf):
-            if tf == 0:
-                x3ps[a] = bank(X_BANK[a], [P, 4, P], "x3ps%d" % a)
+        def x_pass(h, tf, g):
+            if g == 0:
+                x3ps[(h, tf)] = bank(X_BANK[h][tf], [P, 512], "x3ps%d_%d" % (h, tf))
             fs = slice(P * tf, P * tf + P)
-            for g in range(2):
-                nc.tensor.matmul_mx(
-                    out=x3ps[a][:, tf, :],
-                    lhsT=cs[g][:, fs].bitcast(FP8X4),
-                    lhsT_scale=ss[g][:, fs],
-                    rhs=codes[4 + a][:, P * g : P * g + P].bitcast(FP8X4),
-                    rhs_scale=scales[4 + a][:, P * g : P * g + P],
-                    start=(g == 0),
-                    stop=(g == 1),
-                )
+            ns = slice(512 * h, 512 * h + 512)
+            nc.tensor.matmul_mx(
+                out=x3ps[(h, tf)][:],
+                lhsT=cs[g][:, fs].bitcast(FP8X4),
+                lhsT_scale=ss[g][:, fs],
+                rhs=ca[g][:, ns].bitcast(FP8X4),
+                rhs_scale=sa[g][:, ns],
+                start=(g == 0),
+                stop=(g == 1),
+            )
 
-        def x_evac_scalar(a):
-            pl = work.tile([P, 4, P], BF16, tag="x3pl", name="x3pl%d" % a)
-            for tf in range(4):
+        def x_evac(eng, h, tf):
+            if eng == "s":
                 nc.scalar.activation(
-                    out=pl[:, tf, :],
-                    in_=x3ps[a][:, tf, :],
+                    out=pl3[h][:, tf, :],
+                    in_=x3ps[(h, tf)][:],
                     func=ACT.Identity,
                     bias=consts[:, 0, tf : tf + 1],
                     scale=1.0,
                 )
-            return pl
+            else:
+                nc.vector.tensor_scalar(
+                    out=pl3[h][:, tf, :],
+                    in0=x3ps[(h, tf)][:],
+                    scalar1=consts[:, 0, tf : tf + 1],
+                    scalar2=None,
+                    op0=ALU.add,
+                )
 
-        def x_regroup(a, pl):
-            gx3[a] = keep.tile([P, P, 4], BF16, name="gx3_%d" % a, align_bytes=64)
-            nc.vector.tensor_copy(
-                out=gx3[a][:].rearrange("p (c i) t -> p c t i", i=4),
-                in_=pl[:].rearrange("p t (c i) -> p c t i", i=4),
-            )
-
-        def x_evac_vector(a):
-            gx3[a] = keep.tile([P, P, 4], BF16, name="gx3_%d" % a, align_bytes=64)
-            nc.vector.tensor_tensor(
-                out=gx3[a][:],
-                in0=x3ps[a][:].rearrange("p t m -> p m t"),
-                in1=consts[:, 0, 0:4].unsqueeze(1).to_broadcast([P, P, 4]),
-                op=ALU.add,
-            )
+        def x_regroup(eng, a):
+            h, ms = a // 4, slice(P * (a % 4), P * (a % 4) + P)
+            regroup(eng, gx3[h][:, ms, :], pl3[h][:, :, ms])
 
         def x_quant(a):
-            c3[a] = keep.tile([P, P], U32, name="c3_%d" % a, align_bytes=64)
-            s3[a] = keep.tile([P, P], U8, name="s3_%d" % a, align_bytes=64)
+            h, ms = a // 4, slice(P * (a % 4), P * (a % 4) + P)
             nc.vector.quantize_mx(
-                out=c3[a][:].bitcast(FP8X4), scales=s3[a][:], in_=gx3[a][:].rearrange("p m t -> p (m t)")
+                out=c3[h][:, ms].bitcast(FP8X4),
+                scales=s3[h][:, ms],
+                in_=gx3[h][:, ms, :].rearrange("p m t -> p (m t)"),
             )
 
         def logits(a):
-            l3[a] = bank(L_BANK[a % 2], [P, P], "l3_%d" % a)
-            cols = slice(P * (a % 2), P * (a % 2) + P)
-            parts = (
-                (codes[12 + a // 2][:, cols], scales[12 + a // 2][:, cols]),
-                (codes[a // 2][:, cols], scales[a // 2][:, cols]),
-                (c3[a][:], s3[a][:]),
-            )
+            l3[a] = bank(L_BANK[a % 4], [P, P], "l3_%d" % a)
+            cols = slice(P * a, P * a + P)
+            h, ms = a // 4, slice(P * (a % 4), P * (a % 4) + P)
+            parts = ((cx1[:, cols], sx1[:, cols]), (cx2[:, cols], sx2[:, cols]), (c3[h][:, ms], s3[h][:, ms]))
             for c in range(3):
                 nc.tensor.matmul_mx(
                     out=l3[a][:],
@@ -305,45 +350,59 @@ def tile_gcn_pb_kernel(tc, x1, x2, adj, W3, b3, Wl, bl, out):
             )
 
         for tf in range(4):
-            for a in range(4):
-                x_pass(a, tf)
+            x_pass(0, tf, 0)
+        for tf in range(4):
+            x_pass(0, tf, 1)
+        for tf in range(4):
+            x_pass(1, tf, 0)
+            x_pass(1, tf, 1)
+        x_evac("v", 0, 0)
+        x_evac("s", 0, 1)
         quant_t(12)
+        x_evac("v", 0, 2)
+        x_evac("s", 0, 3)
         quant_t(13)
-        x_evac_vector(0)
-        pl1 = x_evac_scalar(1)
-        pl3 = x_evac_scalar(3)
-        x_quant(0)
         quant_t(14)
         quant_t(15)
-        x_evac_vector(2)
-        for tf in range(4):
-            x_pass(4, tf)
-        logits(0)
-        z_max(0)
-        exp_sum(0)
-        x_regroup(1, pl1)
+        x_regroup("v", 0)
+        x_regroup("s", 1)
+        x_quant(0)
         x_quant(1)
+        x_evac("s", 1, 0)
+        x_regroup("v", 2)
+        x_regroup("s", 3)
         x_quant(2)
-        x_regroup(3, pl3)
-        x_quant(3)
+        x_evac("v", 1, 1)
+        x_evac("s", 1, 2)
+        x_evac("s", 1, 3)
+        logits(0)
         logits(1)
         logits(2)
+        z_max(0)
+        exp_sum(0)
+        x_regroup("s", 5)
         z_max(1)
         exp_sum(1)
+        x_regroup("s", 7)
+        x_quant(3)
+        logits(3)
+        x_regroup("v", 4)
         z_max(2)
         exp_sum(2)
-        for a in range(4, 8):
-            if a < 7:
-                for tf in range(4):
-                    x_pass(a + 1, tf)
-            logits(a - 1)
-            x_evac_vector(a)
-            z_max(a - 1)
-            exp_sum(a - 1)
-            x_quant(a)
+        x_quant(4)
+        x_quant(5)
+        logits(4)
+        logits(5)
+        x_regroup("v", 6)
+        z_max(3)
+        exp_sum(3)
+        x_quant(6)
+        x_quant(7)
+        logits(6)
         logits(7)
-        z_max(7)
-        exp_sum(7)
+        for a in range(4, 8):
+            z_max(a)
+            exp_sum(a)
 
         logs = keep.tile([P, 8], F32, name="logs")
         nc.scalar.activation(out=logs[:], in_=sums[:], func=ACT.Ln)

@@ -16,9 +16,9 @@ P = 128
 FLOPS = 2 * 1024 * 512 * 512 + 2 * 1024 * 1024 * 512 + 2 * 1024 * 1536 * 128
 
 N_T_BANKS = 5
-V_EVAC = (0, 3, 5, 7, 13, 14)
+V_EVAC = (0, 3, 5, 7, 9)
 X_BANK = ((7, 5, 1, 6), (2, 3, 4, 0))
-L_BANK = (7, 5, 1, 6)
+L_BANK = (7, 5, 7, 5)
 
 
 def tile_gcn_pb_kernel(tc, x1, x2, adj, W3, b3, Wl, bl, out):
@@ -79,7 +79,9 @@ def tile_gcn_pb_kernel(tc, x1, x2, adj, W3, b3, Wl, bl, out):
         adjw = adj_sb[:].bitcast(F32)
 
         tps = {}
-        grouped = {}
+        gx2 = keep.tile([P, 1024, 4], BF16, name="gx2", align_bytes=64)
+        gx1 = keep.tile([P, 1024, 4], BF16, name="gx1", align_bytes=64)
+        ga = [keep.tile([P, 1024, 4], BF16, name="ga%d" % g, align_bytes=64) for g in range(2)]
         cx2 = keep.tile([P, 1024], U32, name="cx2", align_bytes=64)
         sx2 = keep.tile([P, 1024], U8, name="sx2", align_bytes=64)
         cx1 = keep.tile([P, 1024], U32, name="cx1", align_bytes=64)
@@ -102,25 +104,23 @@ def tile_gcn_pb_kernel(tc, x1, x2, adj, W3, b3, Wl, bl, out):
             nc.tensor.transpose(tps[k][:, j, :], t_in(k, j), ident[:])
 
         def evac_t(k):
-            grouped[k] = keep.tile([P, 2, P, 4], BF16, name="grouped%d" % k, align_bytes=64)
-            o = grouped[k][:].bitcast(F32)
+            if k < 4:
+                dst, q = gx2, k
+            elif k < 12:
+                dst, q = ga[(k - 4) % 2], (k - 4) // 2
+            else:
+                dst, q = gx1, k - 12
+            o = dst[:, 256 * q : 256 * q + 256, :].bitcast(F32).rearrange("p (a m) u -> p a m u", a=2)
             i = tps[k][:].rearrange("p (a u) m -> p a m u", a=2)
             if k in V_EVAC:
                 nc.vector.tensor_copy(out=o, in_=i)
             else:
                 nc.scalar.copy(out=o, in_=i)
 
-        def quant_t(k):
-            if k < 4:
-                c, s, q = cx2, sx2, k
-            elif k < 12:
-                c, s, q = ca[(k - 4) % 2], sa[(k - 4) % 2], (k - 4) // 2
-            else:
-                c, s, q = cx1, sx1, k - 12
+        def quant_half(g, c, s, h):
+            ns = slice(512 * h, 512 * h + 512)
             nc.vector.quantize_mx(
-                out=c[:, 256 * q : 256 * q + 256].bitcast(FP8X4),
-                scales=s[:, 256 * q : 256 * q + 256],
-                in_=grouped[k][:].rearrange("p a m t -> p (a m t)"),
+                out=c[:, ns].bitcast(FP8X4), scales=s[:, ns], in_=g[:, ns, :].rearrange("p n t -> p (n t)")
             )
 
         planes = [keep.tile([P, 4, 512], BF16, name="planes%d" % g) for g in range(2)]
@@ -137,8 +137,8 @@ def tile_gcn_pb_kernel(tc, x1, x2, adj, W3, b3, Wl, bl, out):
             else:
                 nc.scalar.copy(out=o, in_=i)
 
-        def regroup_s(eng, g, f0, nf):
-            regroup(eng, gs[g][:, f0 : f0 + nf, :], planes[g][:, :, f0 : f0 + nf])
+        def regroup_s(g, f0, nf):
+            regroup("v", gs[g][:, f0 : f0 + nf, :], planes[g][:, :, f0 : f0 + nf])
 
         def quant_s(g, f0, nf):
             nc.vector.quantize_mx(
@@ -152,7 +152,7 @@ def tile_gcn_pb_kernel(tc, x1, x2, adj, W3, b3, Wl, bl, out):
             for tk in range(4):
                 nc.tensor.matmul(
                     out=accs[i][:],
-                    lhsT=grouped[i // 2][:, i % 2, :, tk],
+                    lhsT=gx2[:, P * i : P * i + P, tk],
                     rhs=w3_sb[:, tk, :],
                     start=(tk == 0),
                     stop=(tk == 3),
@@ -166,24 +166,27 @@ def tile_gcn_pb_kernel(tc, x1, x2, adj, W3, b3, Wl, bl, out):
             if i < 7:
                 nc.scalar.copy(out=planes[i // 4][:, i % 4, :], in_=accs[i][:])
             else:
-                for c in range(4):
+                for c in range(2):
                     nc.scalar.copy(
-                        out=planes[1][:, 3, P * c : P * c + P], in_=accs[i][:, P * c : P * c + P]
+                        out=planes[1][:, 3, 256 * c : 256 * c + 256], in_=accs[i][:, 256 * c : 256 * c + 256]
                     )
 
         gw = keep.tile([P, 3, P, 4], BF16, name="gw", align_bytes=64)
         cw = keep.tile([P, 3, P], U32, name="cw", align_bytes=64)
         sw = keep.tile([P, 3, P], U8, name="sw", align_bytes=64)
 
-        def wl_quant():
-            for c in range(3):
-                regroup("v", gw[:, c], wl_sb[:, 4 * c : 4 * c + 4, :])
-            for c in range(3):
-                nc.vector.quantize_mx(
-                    out=cw[:, c, :].bitcast(FP8X4),
-                    scales=sw[:, c, :],
-                    in_=gw[:, c].rearrange("p n t -> p (n t)"),
-                )
+        def wl_regroup():
+            nc.vector.tensor_copy(
+                out=gw[:].rearrange("p c (n i) t -> p c n t i", i=4),
+                in_=wl_sb[:].rearrange("p (c t) (n i) -> p c n t i", t=4, i=4),
+            )
+
+        def wl_quant(c0, nch):
+            nc.vector.quantize_mx(
+                out=cw[:, c0 : c0 + nch, :].rearrange("p c n -> p (c n)").bitcast(FP8X4),
+                scales=sw[:, c0 : c0 + nch, :].rearrange("p c n -> p (c n)"),
+                in_=gw[:, c0 : c0 + nch].rearrange("p c n t -> p (c n t)"),
+            )
 
         for j in range(4):
             transpose(0, j)
@@ -201,73 +204,65 @@ def tile_gcn_pb_kernel(tc, x1, x2, adj, W3, b3, Wl, bl, out):
 
         support_matmuls(0)
         evac_s(0)
-        quant_t(0)
-        quant_t(1)
-        wl_quant()
+        quant_half(gx2, cx2, sx2, 0)
+        wl_regroup()
 
         support_matmuls(1)
         evac_t(2)
         evac_s(1)
         evac_t(3)
+        wl_quant(0, 2)
+        wl_quant(2, 1)
 
         support_matmuls(2)
         evac_t(4)
         evac_s(2)
         evac_t(5)
-        quant_t(4)
 
         support_matmuls(3)
         evac_t(6)
         evac_s(3)
         evac_t(7)
-        quant_t(5)
-        quant_t(6)
+        quant_half(ga[0], ca[0], sa[0], 0)
+        quant_half(ga[1], ca[1], sa[1], 0)
 
         support_matmuls(4)
         evac_t(8)
         evac_s(4)
         evac_t(9)
-        regroup_s("v", 0, 0, 512)
+        regroup_s(0, 0, 512)
         quant_s(0, 0, 512)
-        quant_t(7)
 
         support_matmuls(5)
         evac_t(10)
         evac_s(5)
         evac_t(11)
-        quant_t(8)
-        quant_t(9)
-        quant_t(2)
+        quant_half(gx2, cx2, sx2, 1)
 
         support_matmuls(6)
-        evac_t(12)
         evac_s(6)
-        quant_t(10)
-        quant_t(11)
-        evac_t(13)
-        quant_t(3)
+        evac_t(12)
+        quant_half(ga[0], ca[0], sa[0], 1)
+        quant_half(ga[1], ca[1], sa[1], 1)
 
         support_matmuls(7)
         evac_s(7)
-        regroup_s("s", 1, P, P)
-        regroup_s("s", 1, 3 * P, P)
-        evac_t(15)
+        regroup_s(1, 0, 256)
+        regroup_s(1, 256, 256)
+        quant_s(1, 0, 256)
+        quant_s(1, 256, 256)
+        evac_t(13)
         evac_t(14)
-        regroup_s("v", 1, 0, P)
-        quant_s(1, 0, P)
-        regroup_s("v", 1, 2 * P, P)
-        quant_s(1, P, P)
-        quant_s(1, 2 * P, P)
-        quant_s(1, 3 * P, P)
+        evac_t(15)
 
         z = keep.tile([P, 8, P], F32, name="z")
         res = keep.tile([P, 8, P], F32, name="res")
         negmax = keep.tile([P, 8], F32, name="negmax")
         sums = keep.tile([P, 8], F32, name="sums")
         pl3 = [keep.tile([P, 4, 512], BF16, name="pl3_%d" % h) for h in range(2)]
-        gx3 = [keep.tile([P, 512, 4], BF16, name="gx3_%d" % h, align_bytes=64) for h in range(2)]
-        c3 = [keep.tile([P, 512], U32, name="c3_%d" % h, align_bytes=64) for h in range(2)]
-        s3 = [keep.tile([P, 512], U8, name="s3_%d" % h, align_bytes=64) for h in range(2)]
+        gx3 = keep.tile([P, 1024, 4], BF16, name="gx3", align_bytes=64)
+        c3 = keep.tile([P, 1024], U32, name="c3", align_bytes=64)
+        s3 = keep.tile([P, 1024], U8, name="s3", align_bytes=64)
         x3ps = {}
         l3 = {}
 
@@ -304,38 +299,41 @@ def tile_gcn_pb_kernel(tc, x1, x2, adj, W3, b3, Wl, bl, out):
                     op0=ALU.add,
                 )
 
-        def x_regroup(eng, a):
-            h, ms = a // 4, slice(P * (a % 4), P * (a % 4) + P)
-            regroup(eng, gx3[h][:, ms, :], pl3[h][:, :, ms])
+        def x_regroup(eng, q):
+            h, m0 = q // 2, 256 * (q % 2)
+            regroup(eng, gx3[:, 256 * q : 256 * q + 256, :], pl3[h][:, :, m0 : m0 + 256])
 
-        def x_quant(a):
-            h, ms = a // 4, slice(P * (a % 4), P * (a % 4) + P)
+        def x_quant(q):
+            ns = slice(256 * q, 256 * q + 256)
             nc.vector.quantize_mx(
-                out=c3[h][:, ms].bitcast(FP8X4),
-                scales=s3[h][:, ms],
-                in_=gx3[h][:, ms, :].rearrange("p m t -> p (m t)"),
+                out=c3[:, ns].bitcast(FP8X4), scales=s3[:, ns], in_=gx3[:, ns, :].rearrange("p m t -> p (m t)")
             )
 
-        def logits(a):
-            l3[a] = bank(L_BANK[a % 4], [P, P], "l3_%d" % a)
-            cols = slice(P * a, P * a + P)
-            h, ms = a // 4, slice(P * (a % 4), P * (a % 4) + P)
-            parts = ((cx1[:, cols], sx1[:, cols]), (cx2[:, cols], sx2[:, cols]), (c3[h][:, ms], s3[h][:, ms]))
-            for c in range(3):
-                nc.tensor.matmul_mx(
-                    out=l3[a][:],
-                    lhsT=parts[c][0].bitcast(FP8X4),
-                    lhsT_scale=parts[c][1],
-                    rhs=cw[:, c, :].bitcast(FP8X4),
-                    rhs_scale=sw[:, c, :],
-                    start=(c == 0),
-                    stop=(c == 2),
-                )
+        def logits(q):
+            l3[q] = bank(L_BANK[q], [P, 2, P], "l3_%d" % q)
+            for a in (2 * q, 2 * q + 1):
+                cols = slice(P * a, P * a + P)
+                parts = ((cx1, sx1), (cx2, sx2), (c3, s3))
+                for c in range(3):
+                    nc.tensor.matmul_mx(
+                        out=l3[q][:, a % 2, :],
+                        lhsT=parts[c][0][:, cols].bitcast(FP8X4),
+                        lhsT_scale=parts[c][1][:, cols],
+                        rhs=cw[:, c, :].bitcast(FP8X4),
+                        rhs_scale=sw[:, c, :],
+                        start=(c == 0),
+                        stop=(c == 2),
+                    )
 
-        def z_max(a):
-            nc.vector.tensor_tensor(out=z[:, a, :], in0=l3[a][:], in1=consts[:, 1, :], op=ALU.add)
+        def z_max(q):
+            nc.vector.tensor_tensor(
+                out=z[:, 2 * q : 2 * q + 2, :],
+                in0=l3[q][:],
+                in1=consts[:, 1, :].unsqueeze(1).to_broadcast([P, 2, P]),
+                op=ALU.add,
+            )
             nc.vector.tensor_reduce(
-                out=negmax[:, a : a + 1], in_=z[:, a, :], axis=AX.X, op=ALU.max, negate=True
+                out=negmax[:, 2 * q : 2 * q + 2], in_=z[:, 2 * q : 2 * q + 2, :], axis=AX.X, op=ALU.max, negate=True
             )
 
         def exp_sum(a):
@@ -356,52 +354,33 @@ def tile_gcn_pb_kernel(tc, x1, x2, adj, W3, b3, Wl, bl, out):
         for tf in range(4):
             x_pass(1, tf, 0)
             x_pass(1, tf, 1)
-        x_evac("v", 0, 0)
-        x_evac("s", 0, 1)
-        quant_t(12)
-        x_evac("v", 0, 2)
-        x_evac("s", 0, 3)
-        quant_t(13)
-        quant_t(14)
-        quant_t(15)
+        quant_half(gx1, cx1, sx1, 0)
+        x_evac("s", 0, 0)
+        x_evac("v", 0, 1)
+        x_evac("s", 0, 2)
+        x_evac("v", 0, 3)
+        quant_half(gx1, cx1, sx1, 1)
+        for tf in range(4):
+            x_evac("s", 1, tf)
         x_regroup("v", 0)
-        x_regroup("s", 1)
         x_quant(0)
-        x_quant(1)
-        x_evac("s", 1, 0)
-        x_regroup("v", 2)
-        x_regroup("s", 3)
-        x_quant(2)
-        x_evac("v", 1, 1)
-        x_evac("s", 1, 2)
-        x_evac("s", 1, 3)
         logits(0)
+        x_regroup("v", 1)
+        x_quant(1)
         logits(1)
-        logits(2)
+        x_regroup("s", 2)
+        x_regroup("s", 3)
         z_max(0)
-        exp_sum(0)
-        x_regroup("s", 5)
         z_max(1)
-        exp_sum(1)
-        x_regroup("s", 7)
+        x_quant(2)
+        logits(2)
         x_quant(3)
         logits(3)
-        x_regroup("v", 4)
+        for a in range(4):
+            exp_sum(a)
         z_max(2)
-        exp_sum(2)
-        x_quant(4)
-        x_quant(5)
-        logits(4)
-        logits(5)
-        x_regroup("v", 6)
         z_max(3)
-        exp_sum(3)
-        x_quant(6)
-        x_quant(7)
-        logits(6)
-        logits(7)
         for a in range(4, 8):
-            z_max(a)
             exp_sum(a)
 
         logs = keep.tile([P, 8], F32, name="logs")
@@ -409,18 +388,15 @@ def tile_gcn_pb_kernel(tc, x1, x2, adj, W3, b3, Wl, bl, out):
         shift = keep.tile([P, 8], F32, name="shift")
         nc.vector.tensor_tensor(out=shift[:], in0=negmax[:], in1=logs[:], op=ALU.subtract)
         out_v = out.rearrange("(s m e) c -> m s e c", s=4, m=P, e=2)
-        for a in range(8):
-            if a % 2 == 0:
-                nc.vector.tensor_scalar(
-                    out=res[:, a, :], in0=z[:, a, :], scalar1=shift[:, a : a + 1], scalar2=None, op0=ALU.add
-                )
-            else:
-                nc.scalar.activation(
-                    out=res[:, a, :], in_=z[:, a, :], func=ACT.Identity, bias=shift[:, a : a + 1], scale=1.0
-                )
-            if a % 4 == 3:
-                h = a // 4
-                nc.sync.dma_start(
-                    out=out_v[:, 2 * h : 2 * h + 2],
-                    in_=res[:, 4 * h : 4 * h + 4, :].rearrange("p (s e) c -> p s e c", e=2),
-                )
+        nc.vector.tensor_tensor(
+            out=res[:, 0:4, :],
+            in0=z[:, 0:4, :],
+            in1=shift[:, 0:4].unsqueeze(2).to_broadcast([P, 4, P]),
+            op=ALU.add,
+        )
+        nc.sync.dma_start(out=out_v[:, 0:2], in_=res[:, 0:4, :].rearrange("p (s e) c -> p s e c", e=2))
+        for a in range(4, 8):
+            nc.scalar.activation(
+                out=res[:, a, :], in_=z[:, a, :], func=ACT.Identity, bias=shift[:, a : a + 1], scale=1.0
+            )
+        nc.sync.dma_start(out=out_v[:, 2:4], in_=res[:, 4:8, :].rearrange("p (s e) c -> p s e c", e=2))

@@ -17,8 +17,8 @@ FLOPS = 2 * 1024 * 512 * 512 + 2 * 1024 * 1024 * 512 + 2 * 1024 * 1536 * 128
 
 N_T_BANKS = 5
 V_EVAC = (0, 3, 5, 7, 9)
-X_BANK = ((7, 5, 1, 6), (2, 3, 4, 0))
-L_BANK = (7, 5, 7, 5)
+X_BANK = ((5, 6, 1, 7), (2, 3, 4, 0))
+L_BANK = (5, 6, 5, 6)
 
 
 def tile_gcn_pb_kernel(tc, x1, x2, adj, W3, b3, Wl, bl, out):
@@ -148,7 +148,7 @@ def tile_gcn_pb_kernel(tc, x1, x2, adj, W3, b3, Wl, bl, out):
             )
 
         def support_matmuls(i):
-            accs[i] = bank(5 + i % 3, [P, 512], "acc%d" % i)
+            accs[i] = bank(5 + (i if i < 3 else i + 1) % 3, [P, 512], "acc%d" % i)
             for tk in range(4):
                 nc.tensor.matmul(
                     out=accs[i][:],
@@ -190,17 +190,11 @@ def tile_gcn_pb_kernel(tc, x1, x2, adj, W3, b3, Wl, bl, out):
 
         for j in range(4):
             transpose(0, j)
-        cps = bank(7, [P, 2, P], "cps")
-        nc.tensor.matmul(out=cps[:, 0, :], lhsT=zrows[:], rhs=ident_bf[:], start=True, stop=True)
-        nc.tensor.matmul(
-            out=cps[:, 1, :], lhsT=ident_bf[:, 4:5].to_broadcast([P, P]), rhs=zrows[:], start=True, stop=True
-        )
         for j in range(4):
             transpose(1, j)
         evac_t(0)
         evac_t(1)
         consts = keep.tile([P, 2, P], F32, name="consts")
-        nc.vector.tensor_copy(out=consts[:], in_=cps[:])
 
         support_matmuls(0)
         evac_s(0)
@@ -219,10 +213,16 @@ def tile_gcn_pb_kernel(tc, x1, x2, adj, W3, b3, Wl, bl, out):
         evac_s(2)
         evac_t(5)
 
+        cps = bank(5, [P, 2, P], "cps")
+        nc.tensor.matmul(out=cps[:, 0, :], lhsT=zrows[:], rhs=ident_bf[:], start=True, stop=True)
+        nc.tensor.matmul(
+            out=cps[:, 1, :], lhsT=ident_bf[:, 4:5].to_broadcast([P, P]), rhs=zrows[:], start=True, stop=True
+        )
         support_matmuls(3)
         evac_t(6)
         evac_s(3)
         evac_t(7)
+        nc.vector.tensor_copy(out=consts[:], in_=cps[:])
         quant_half(ga[0], ca[0], sa[0], 0)
         quant_half(ga[1], ca[1], sa[1], 0)
 

@@ -16,7 +16,8 @@ P = 128
 FLOPS = 2 * 1024 * 512 * 512 + 2 * 1024 * 1024 * 512 + 2 * 1024 * 1536 * 128
 
 N_T_BANKS = 5
-V_EVAC = (0, 3, 5, 7, 9)
+V_EVAC = (0, 3, 7, 11)
+WOVEN = (1, 2, 2, 4, 6, 8, 10, 12, 13)
 X_BANK = ((5, 6, 1, 7), (2, 3, 4, 0))
 L_BANK = (5, 6, 5, 6)
 
@@ -45,6 +46,8 @@ def tile_gcn_pb_kernel(tc, x1, x2, adj, W3, b3, Wl, bl, out):
         make_identity(nc, ident[:])
         zrows = keep.tile([P, P], BF16, name="zrows")
         nc.vector.memset(zrows[:], 0.0)
+        warm = keep.tile([P, 512], BF16, name="warm")
+        nc.vector.memset(warm[:], 0.0)
         ident_bf = keep.tile([P, P], BF16, name="ident_bf")
         nc.vector.tensor_copy(out=ident_bf[:], in_=ident[:])
         nc.scalar.dma_start(out=zrows[0:4, :], in_=b3.rearrange("(r c) -> r c", r=4))
@@ -61,7 +64,6 @@ def tile_gcn_pb_kernel(tc, x1, x2, adj, W3, b3, Wl, bl, out):
             in_=W3.rearrange("(u q e) c -> q u e c", u=2, q=P, e=2),
         )
         load_nodes(x2_sb, x2, 1, 1)
-        load_nodes(x2_sb, x2, 2, 2)
         nc.sync.dma_start(
             out=wl_sb[:, 0:8, :].rearrange("p (cu e) n -> p cu e n", e=2),
             in_=Wl[0:1024, :].rearrange("(cu q e) n -> q cu e n", cu=4, q=P, e=2),
@@ -69,6 +71,7 @@ def tile_gcn_pb_kernel(tc, x1, x2, adj, W3, b3, Wl, bl, out):
         nc.sync.dma_start(
             out=wl_sb[:, 8:12, :], in_=Wl[1024:1536, :].rearrange("(t p) n -> p t n", t=4, p=P)
         )
+        load_nodes(x2_sb, x2, 2, 2)
         for s in range(4):
             load_nodes(adj_sb, adj, s, 1)
         load_nodes(x1_sb, x1, 0, 2)
@@ -147,6 +150,13 @@ def tile_gcn_pb_kernel(tc, x1, x2, adj, W3, b3, Wl, bl, out):
                 in_=gs[g][:, f0 : f0 + nf, :].rearrange("p f t -> p (f t)"),
             )
 
+        def woven(i, tk):
+            banks = range(WOVEN[i], WOVEN[i + 1])
+            todo = [(k, j) for k in banks for j in range(4)]
+            if len(todo) == 4:
+                return todo[2 * tk - 4 : 2 * tk - 2] if tk >= 2 else []
+            return todo[2 * tk : 2 * tk + 2]
+
         def support_matmuls(i):
             accs[i] = bank(5 + (i if i < 3 else i + 1) % 3, [P, 512], "acc%d" % i)
             for tk in range(4):
@@ -157,10 +167,8 @@ def tile_gcn_pb_kernel(tc, x1, x2, adj, W3, b3, Wl, bl, out):
                     start=(tk == 0),
                     stop=(tk == 3),
                 )
-                if i > 0:
-                    k = 2 * i + tk // 2
-                    transpose(k, 2 * (tk % 2))
-                    transpose(k, 2 * (tk % 2) + 1)
+                for k, j in woven(i, tk):
+                    transpose(k, j)
 
         def evac_s(i):
             if i < 7:
@@ -188,30 +196,29 @@ def tile_gcn_pb_kernel(tc, x1, x2, adj, W3, b3, Wl, bl, out):
                 in_=gw[:, c0 : c0 + nch].rearrange("p c n t -> p (c n t)"),
             )
 
+        wps = bank(5, [P, 512], "wps")
+        for n in range(4):
+            nc.tensor.matmul(out=wps[:], lhsT=warm[:, 0:P], rhs=warm[:], start=True, stop=True)
         for j in range(4):
             transpose(0, j)
-        for j in range(4):
-            transpose(1, j)
         evac_t(0)
-        evac_t(1)
         consts = keep.tile([P, 2, P], F32, name="consts")
 
         support_matmuls(0)
+        evac_t(1)
         evac_s(0)
-        quant_half(gx2, cx2, sx2, 0)
-        wl_regroup()
 
         support_matmuls(1)
-        evac_t(2)
         evac_s(1)
-        evac_t(3)
-        wl_quant(0, 2)
-        wl_quant(2, 1)
+        wl_regroup()
 
         support_matmuls(2)
-        evac_t(4)
+        evac_t(2)
+        evac_t(3)
         evac_s(2)
-        evac_t(5)
+        wl_quant(0, 2)
+        wl_quant(2, 1)
+        quant_half(gx2, cx2, sx2, 0)
 
         cps = bank(5, [P, 2, P], "cps")
         nc.tensor.matmul(out=cps[:, 0, :], lhsT=zrows[:], rhs=ident_bf[:], start=True, stop=True)
@@ -219,41 +226,44 @@ def tile_gcn_pb_kernel(tc, x1, x2, adj, W3, b3, Wl, bl, out):
             out=cps[:, 1, :], lhsT=ident_bf[:, 4:5].to_broadcast([P, P]), rhs=zrows[:], start=True, stop=True
         )
         support_matmuls(3)
-        evac_t(6)
+        evac_t(4)
+        evac_t(5)
         evac_s(3)
-        evac_t(7)
         nc.vector.tensor_copy(out=consts[:], in_=cps[:])
-        quant_half(ga[0], ca[0], sa[0], 0)
-        quant_half(ga[1], ca[1], sa[1], 0)
+        quant_half(gx2, cx2, sx2, 1)
 
         support_matmuls(4)
-        evac_t(8)
+        evac_t(6)
+        evac_t(7)
         evac_s(4)
-        evac_t(9)
         regroup_s(0, 0, 512)
+        quant_half(ga[0], ca[0], sa[0], 0)
         quant_s(0, 0, 512)
 
         support_matmuls(5)
-        evac_t(10)
+        evac_t(8)
+        evac_t(9)
         evac_s(5)
-        evac_t(11)
-        quant_half(gx2, cx2, sx2, 1)
+        quant_half(ga[1], ca[1], sa[1], 0)
 
         support_matmuls(6)
+        evac_t(10)
+        evac_t(11)
         evac_s(6)
-        evac_t(12)
         quant_half(ga[0], ca[0], sa[0], 1)
-        quant_half(ga[1], ca[1], sa[1], 1)
 
         support_matmuls(7)
         evac_s(7)
+        quant_half(ga[1], ca[1], sa[1], 1)
         regroup_s(1, 0, 256)
         regroup_s(1, 256, 256)
         quant_s(1, 0, 256)
         quant_s(1, 256, 256)
-        evac_t(13)
-        evac_t(14)
-        evac_t(15)
+        for k in range(13, 16):
+            for j in range(4):
+                transpose(k, j)
+        for k in range(12, 16):
+            evac_t(k)
 
         z = keep.tile([P, 8, P], F32, name="z")
         res = keep.tile([P, 8, P], F32, name="res")
@@ -383,20 +393,30 @@ def tile_gcn_pb_kernel(tc, x1, x2, adj, W3, b3, Wl, bl, out):
         for a in range(4, 8):
             exp_sum(a)
 
-        logs = keep.tile([P, 8], F32, name="logs")
-        nc.scalar.activation(out=logs[:], in_=sums[:], func=ACT.Ln)
-        shift = keep.tile([P, 8], F32, name="shift")
-        nc.vector.tensor_tensor(out=shift[:], in0=negmax[:], in1=logs[:], op=ALU.subtract)
-        out_v = out.rearrange("(s m e) c -> m s e c", s=4, m=P, e=2)
+        rsums = keep.tile([P, 8], F32, name="rsums")
+        nc.vector.reciprocal(out=rsums[:], in_=sums[:])
+        zc = keep.tile([P, 3, P], F32, name="zc")
         nc.vector.tensor_tensor(
-            out=res[:, 0:4, :],
-            in0=z[:, 0:4, :],
-            in1=shift[:, 0:4].unsqueeze(2).to_broadcast([P, 4, P]),
+            out=zc[:],
+            in0=z[:, 5:8, :],
+            in1=negmax[:, 5:8].unsqueeze(2).to_broadcast([P, 3, P]),
             op=ALU.add,
         )
+        nlogs = keep.tile([P, 8], F32, name="nlogs")
+        nc.scalar.activation(out=nlogs[:], in_=rsums[:], func=ACT.Ln)
+        out_v = out.rearrange("(s m e) c -> m s e c", s=4, m=P, e=2)
+        for a in range(5):
+            nc.vector.tensor_scalar(
+                out=res[:, a, :],
+                in0=z[:, a, :],
+                scalar1=negmax[:, a : a + 1],
+                scalar2=nlogs[:, a : a + 1],
+                op0=ALU.add,
+                op1=ALU.add,
+            )
         nc.sync.dma_start(out=out_v[:, 0:2], in_=res[:, 0:4, :].rearrange("p (s e) c -> p s e c", e=2))
-        for a in range(4, 8):
+        for a in range(5, 8):
             nc.scalar.activation(
-                out=res[:, a, :], in_=z[:, a, :], func=ACT.Identity, bias=shift[:, a : a + 1], scale=1.0
+                out=res[:, a, :], in_=zc[:, a - 5, :], func=ACT.Identity, bias=nlogs[:, a : a + 1], scale=1.0
             )
         nc.sync.dma_start(out=out_v[:, 2:4], in_=res[:, 4:8, :].rearrange("p (s e) c -> p s e c", e=2))

@@ -18,8 +18,9 @@ FLOPS = 2 * 1024 * 512 * 512 + 2 * 1024 * 1024 * 512 + 2 * 1024 * 1536 * 128
 N_T_BANKS = 5
 V_EVAC = (0, 3, 7, 11)
 WOVEN = (1, 2, 2, 4, 6, 8, 10, 12, 13)
-X_BANK = ((5, 6, 1, 7), (2, 3, 4, 0))
-L_BANK = (5, 6, 5, 6)
+X_BANK = (5, 6, 1, 7)
+XD_BANK = (2, 3, 4, 0)
+L_BANK = (1, 7, 5, 6)
 
 
 def tile_gcn_pb_kernel(tc, x1, x2, adj, W3, b3, Wl, bl, out):
@@ -250,15 +251,15 @@ def tile_gcn_pb_kernel(tc, x1, x2, adj, W3, b3, Wl, bl, out):
         evac_t(10)
         evac_t(11)
         evac_s(6)
-        quant_half(ga[0], ca[0], sa[0], 1)
 
         support_matmuls(7)
         evac_s(7)
-        quant_half(ga[1], ca[1], sa[1], 1)
         regroup_s(1, 0, 256)
         regroup_s(1, 256, 256)
         quant_s(1, 0, 256)
         quant_s(1, 256, 256)
+        quant_half(ga[0], ca[0], sa[0], 1)
+        quant_half(ga[1], ca[1], sa[1], 1)
         for k in range(13, 16):
             for j in range(4):
                 transpose(k, j)
@@ -269,20 +270,17 @@ def tile_gcn_pb_kernel(tc, x1, x2, adj, W3, b3, Wl, bl, out):
         res = keep.tile([P, 8, P], F32, name="res")
         negmax = keep.tile([P, 8], F32, name="negmax")
         sums = keep.tile([P, 8], F32, name="sums")
-        pl3 = [keep.tile([P, 4, 512], BF16, name="pl3_%d" % h) for h in range(2)]
+        pl3 = keep.tile([P, 4, 512], BF16, name="pl3")
         gx3 = keep.tile([P, 1024, 4], BF16, name="gx3", align_bytes=64)
         c3 = keep.tile([P, 1024], U32, name="c3", align_bytes=64)
         s3 = keep.tile([P, 1024], U8, name="s3", align_bytes=64)
         x3ps = {}
         l3 = {}
 
-        def x_pass(h, tf, g):
-            if g == 0:
-                x3ps[(h, tf)] = bank(X_BANK[h][tf], [P, 512], "x3ps%d_%d" % (h, tf))
+        def x_mm(ps, g, tf, ns):
             fs = slice(P * tf, P * tf + P)
-            ns = slice(512 * h, 512 * h + 512)
             nc.tensor.matmul_mx(
-                out=x3ps[(h, tf)][:],
+                out=ps,
                 lhsT=cs[g][:, fs].bitcast(FP8X4),
                 lhsT_scale=ss[g][:, fs],
                 rhs=ca[g][:, ns].bitcast(FP8X4),
@@ -291,49 +289,63 @@ def tile_gcn_pb_kernel(tc, x1, x2, adj, W3, b3, Wl, bl, out):
                 stop=(g == 1),
             )
 
-        def x_evac(eng, h, tf):
-            if eng == "s":
-                nc.scalar.activation(
-                    out=pl3[h][:, tf, :],
-                    in_=x3ps[(h, tf)][:],
-                    func=ACT.Identity,
-                    bias=consts[:, 0, tf : tf + 1],
-                    scale=1.0,
-                )
-            else:
-                nc.vector.tensor_scalar(
-                    out=pl3[h][:, tf, :],
-                    in0=x3ps[(h, tf)][:],
-                    scalar1=consts[:, 0, tf : tf + 1],
-                    scalar2=None,
-                    op0=ALU.add,
-                )
+        def x_pass(tf, g):
+            if g == 0:
+                x3ps[tf] = bank(X_BANK[tf], [P, 512], "x3ps%d" % tf)
+            x_mm(x3ps[tf][:], g, tf, slice(0, 512))
 
-        def x_regroup(eng, q):
-            h, m0 = q // 2, 256 * (q % 2)
-            regroup(eng, gx3[:, 256 * q : 256 * q + 256, :], pl3[h][:, :, m0 : m0 + 256])
+        def x_evac(tf):
+            nc.scalar.activation(
+                out=pl3[:, tf, :],
+                in_=x3ps[tf][:],
+                func=ACT.Identity,
+                bias=consts[:, 0, tf : tf + 1],
+                scale=1.0,
+            )
 
-        def x_quant(q):
-            ns = slice(256 * q, 256 * q + 256)
+        def x_regroup(q):
+            regroup("s", gx3[:, 256 * q : 256 * q + 256, :], pl3[:, :, 256 * q : 256 * q + 256])
+
+        def xd_pass(a):
+            x3ps[a] = bank(XD_BANK[a - 4], [P, 4, P], "x3ps%d" % a)
+            for tf in range(4):
+                for g in range(2):
+                    x_mm(x3ps[a][:, tf, :], g, tf, slice(P * a, P * a + P))
+
+        def xd_evac(a):
+            nc.vector.tensor_tensor(
+                out=gx3[:, P * a : P * a + P, :],
+                in0=x3ps[a][:].rearrange("p t m -> p m t"),
+                in1=consts[:, 0, 0:4].unsqueeze(1).to_broadcast([P, P, 4]),
+                op=ALU.add,
+            )
+
+        def x_quant(a, na):
+            ns = slice(P * a, P * (a + na))
             nc.vector.quantize_mx(
                 out=c3[:, ns].bitcast(FP8X4), scales=s3[:, ns], in_=gx3[:, ns, :].rearrange("p m t -> p (m t)")
             )
 
+        def logits_tile(a):
+            q = a // 2
+            if a % 2 == 0:
+                l3[q] = bank(L_BANK[q], [P, 2, P], "l3_%d" % q)
+            cols = slice(P * a, P * a + P)
+            parts = ((cx1, sx1), (cx2, sx2), (c3, s3))
+            for c in range(3):
+                nc.tensor.matmul_mx(
+                    out=l3[q][:, a % 2, :],
+                    lhsT=parts[c][0][:, cols].bitcast(FP8X4),
+                    lhsT_scale=parts[c][1][:, cols],
+                    rhs=cw[:, c, :].bitcast(FP8X4),
+                    rhs_scale=sw[:, c, :],
+                    start=(c == 0),
+                    stop=(c == 2),
+                )
+
         def logits(q):
-            l3[q] = bank(L_BANK[q], [P, 2, P], "l3_%d" % q)
             for a in (2 * q, 2 * q + 1):
-                cols = slice(P * a, P * a + P)
-                parts = ((cx1, sx1), (cx2, sx2), (c3, s3))
-                for c in range(3):
-                    nc.tensor.matmul_mx(
-                        out=l3[q][:, a % 2, :],
-                        lhsT=parts[c][0][:, cols].bitcast(FP8X4),
-                        lhsT_scale=parts[c][1][:, cols],
-                        rhs=cw[:, c, :].bitcast(FP8X4),
-                        rhs_scale=sw[:, c, :],
-                        start=(c == 0),
-                        stop=(c == 2),
-                    )
+                logits_tile(a)
 
         def z_max(q):
             nc.vector.tensor_tensor(
@@ -357,40 +369,40 @@ def tile_gcn_pb_kernel(tc, x1, x2, adj, W3, b3, Wl, bl, out):
                 accum_out=sums[:, a : a + 1],
             )
 
+        for g in range(2):
+            for tf in range(4):
+                x_pass(tf, g)
+        for a in range(4, 8):
+            xd_pass(a)
         for tf in range(4):
-            x_pass(0, tf, 0)
-        for tf in range(4):
-            x_pass(0, tf, 1)
-        for tf in range(4):
-            x_pass(1, tf, 0)
-            x_pass(1, tf, 1)
+            x_evac(tf)
+        x_regroup(0)
+        x_regroup(1)
         quant_half(gx1, cx1, sx1, 0)
-        x_evac("s", 0, 0)
-        x_evac("v", 0, 1)
-        x_evac("s", 0, 2)
-        x_evac("v", 0, 3)
         quant_half(gx1, cx1, sx1, 1)
-        for tf in range(4):
-            x_evac("s", 1, tf)
-        x_regroup("v", 0)
-        x_quant(0)
+        xd_evac(4)
+        xd_evac(5)
+        x_quant(4, 1)
+        logits_tile(4)
+        xd_evac(6)
+        x_quant(5, 1)
+        logits_tile(5)
+        xd_evac(7)
+        x_quant(6, 1)
+        logits_tile(6)
+        z_max(2)
+        x_quant(7, 1)
+        logits_tile(7)
+        x_quant(0, 2)
         logits(0)
-        x_regroup("v", 1)
-        x_quant(1)
+        z_max(3)
+        x_quant(2, 2)
         logits(1)
-        x_regroup("s", 2)
-        x_regroup("s", 3)
+        for a in range(4, 8):
+            exp_sum(a)
         z_max(0)
         z_max(1)
-        x_quant(2)
-        logits(2)
-        x_quant(3)
-        logits(3)
         for a in range(4):
-            exp_sum(a)
-        z_max(2)
-        z_max(3)
-        for a in range(4, 8):
             exp_sum(a)
 
         rsums = keep.tile([P, 8], F32, name="rsums")

@@ -16,11 +16,11 @@ P = 128
 FLOPS = 2 * 1024 * 512 * 512 + 2 * 1024 * 1024 * 512 + 2 * 1024 * 1536 * 128
 
 N_T_BANKS = 5
-V_EVAC = (0, 3, 7, 11)
+V_EVAC = (0, 3, 5, 9)
 WOVEN = (1, 2, 2, 4, 6, 8, 10, 12, 13)
 X_BANK = (5, 6, 1, 7)
 XD_BANK = (2, 3, 4, 0)
-L_BANK = (1, 7, 5, 6)
+L_BANK = {0: 1, 1: 2, 2: 6, 3: 7, 4: 5}
 
 
 def tile_gcn_pb_kernel(tc, x1, x2, adj, W3, b3, Wl, bl, out):
@@ -45,10 +45,10 @@ def tile_gcn_pb_kernel(tc, x1, x2, adj, W3, b3, Wl, bl, out):
 
         ident = keep.tile([P, P], F32, name="ident")
         make_identity(nc, ident[:])
+        warm = keep.tile([P, 512], BF16, name="warm")
+        nc.vector.memset(warm[:].bitcast(U32), 0)
         zrows = keep.tile([P, P], BF16, name="zrows")
         nc.vector.memset(zrows[:], 0.0)
-        warm = keep.tile([P, 512], BF16, name="warm")
-        nc.vector.memset(warm[:], 0.0)
         ident_bf = keep.tile([P, P], BF16, name="ident_bf")
         nc.vector.tensor_copy(out=ident_bf[:], in_=ident[:])
         nc.scalar.dma_start(out=zrows[0:4, :], in_=b3.rearrange("(r c) -> r c", r=4))
@@ -59,11 +59,14 @@ def tile_gcn_pb_kernel(tc, x1, x2, adj, W3, b3, Wl, bl, out):
         adj_sb = keep.tile([P, 8, 1024], BF16, name="adj_sb")
         w3_sb = keep.tile([P, 4, 512], BF16, name="w3_sb")
         wl_sb = keep.tile([P, 12, P], BF16, name="wl_sb")
-        load_nodes(x2_sb, x2, 0, 1)
-        nc.sync.dma_start(
-            out=w3_sb[:].rearrange("p (u e) c -> p u e c", e=2),
-            in_=W3.rearrange("(u q e) c -> q u e c", u=2, q=P, e=2),
-        )
+        x2_first = x2[0 : 2 * P, :].rearrange("(m e) k -> m e k", e=2)
+        nc.sync.dma_start(out=x2_sb[:, 0, :], in_=x2_first[:, 0])
+        for u in range(2):
+            nc.sync.dma_start(
+                out=w3_sb[:, 2 * u : 2 * u + 2, :],
+                in_=W3[2 * P * u : 2 * P * (u + 1), :].rearrange("(q e) c -> q e c", e=2),
+            )
+        nc.sync.dma_start(out=x2_sb[:, 1, :], in_=x2_first[:, 1])
         load_nodes(x2_sb, x2, 1, 1)
         nc.sync.dma_start(
             out=wl_sb[:, 0:8, :].rearrange("p (cu e) n -> p cu e n", e=2),
@@ -106,6 +109,19 @@ def tile_gcn_pb_kernel(tc, x1, x2, adj, W3, b3, Wl, bl, out):
             if j == 0:
                 tps[k] = bank(k % N_T_BANKS, [P, 4, P], "tp%d" % k)
             nc.tensor.transpose(tps[k][:, j, :], t_in(k, j), ident[:])
+
+        def transpose_first(a):
+            tps[-1 - a] = bank((0, 4)[a], [P, 2, P], "tpf%d" % a)
+            for u in range(2):
+                nc.tensor.transpose(tps[-1 - a][:, u, :], t_in(0, 2 * a + u), ident[:])
+
+        def evac_first(a):
+            o = gx2[:, P * a : P * a + P, :].bitcast(F32)
+            i = tps[-1 - a][:].rearrange("p u m -> p m u")
+            if a == 0:
+                nc.vector.tensor_copy(out=o, in_=i)
+            else:
+                nc.scalar.copy(out=o, in_=i)
 
         def evac_t(k):
             if k < 4:
@@ -152,6 +168,8 @@ def tile_gcn_pb_kernel(tc, x1, x2, adj, W3, b3, Wl, bl, out):
             )
 
         def woven(i, tk):
+            if i == 0:
+                return []
             banks = range(WOVEN[i], WOVEN[i + 1])
             todo = [(k, j) for k in banks for j in range(4)]
             if len(todo) == 4:
@@ -168,8 +186,13 @@ def tile_gcn_pb_kernel(tc, x1, x2, adj, W3, b3, Wl, bl, out):
                     start=(tk == 0),
                     stop=(tk == 3),
                 )
+                if i == 0 and tk == 1:
+                    transpose_first(1)
                 for k, j in woven(i, tk):
                     transpose(k, j)
+            if i == 0:
+                for j in range(4):
+                    transpose(1, j)
 
         def evac_s(i):
             if i < 7:
@@ -184,10 +207,10 @@ def tile_gcn_pb_kernel(tc, x1, x2, adj, W3, b3, Wl, bl, out):
         cw = keep.tile([P, 3, P], U32, name="cw", align_bytes=64)
         sw = keep.tile([P, 3, P], U8, name="sw", align_bytes=64)
 
-        def wl_regroup():
+        def wl_regroup(c0, nch):
             nc.vector.tensor_copy(
-                out=gw[:].rearrange("p c (n i) t -> p c n t i", i=4),
-                in_=wl_sb[:].rearrange("p (c t) (n i) -> p c n t i", t=4, i=4),
+                out=gw[:, c0 : c0 + nch].rearrange("p c (n i) t -> p c n t i", i=4),
+                in_=wl_sb[:, 4 * c0 : 4 * (c0 + nch), :].rearrange("p (c t) (n i) -> p c n t i", t=4, i=4),
             )
 
         def wl_quant(c0, nch):
@@ -200,32 +223,34 @@ def tile_gcn_pb_kernel(tc, x1, x2, adj, W3, b3, Wl, bl, out):
         wps = bank(5, [P, 512], "wps")
         for n in range(4):
             nc.tensor.matmul(out=wps[:], lhsT=warm[:, 0:P], rhs=warm[:], start=True, stop=True)
-        for j in range(4):
-            transpose(0, j)
-        evac_t(0)
+        transpose_first(0)
+        evac_first(0)
         consts = keep.tile([P, 2, P], F32, name="consts")
 
         support_matmuls(0)
+        evac_first(1)
         evac_t(1)
         evac_s(0)
 
         support_matmuls(1)
         evac_s(1)
-        wl_regroup()
+        wl_regroup(0, 2)
+        wl_regroup(2, 1)
+        quant_half(gx2, cx2, sx2, 0)
+        wl_quant(0, 2)
+        wl_quant(2, 1)
 
         support_matmuls(2)
         evac_t(2)
         evac_t(3)
         evac_s(2)
-        wl_quant(0, 2)
-        wl_quant(2, 1)
-        quant_half(gx2, cx2, sx2, 0)
 
         cps = bank(5, [P, 2, P], "cps")
         nc.tensor.matmul(out=cps[:, 0, :], lhsT=zrows[:], rhs=ident_bf[:], start=True, stop=True)
         nc.tensor.matmul(
             out=cps[:, 1, :], lhsT=ident_bf[:, 4:5].to_broadcast([P, P]), rhs=zrows[:], start=True, stop=True
         )
+
         support_matmuls(3)
         evac_t(4)
         evac_t(5)
@@ -251,6 +276,7 @@ def tile_gcn_pb_kernel(tc, x1, x2, adj, W3, b3, Wl, bl, out):
         evac_t(10)
         evac_t(11)
         evac_s(6)
+        quant_half(ga[0], ca[0], sa[0], 1)
 
         support_matmuls(7)
         evac_s(7)
@@ -258,13 +284,17 @@ def tile_gcn_pb_kernel(tc, x1, x2, adj, W3, b3, Wl, bl, out):
         regroup_s(1, 256, 256)
         quant_s(1, 0, 256)
         quant_s(1, 256, 256)
-        quant_half(ga[0], ca[0], sa[0], 1)
         quant_half(ga[1], ca[1], sa[1], 1)
-        for k in range(13, 16):
-            for j in range(4):
-                transpose(k, j)
-        for k in range(12, 16):
-            evac_t(k)
+        for j in range(4):
+            transpose(13, j)
+        for j in range(4):
+            transpose(14, j)
+        for j in range(4):
+            transpose(15, j)
+        evac_t(12)
+        evac_t(13)
+        evac_t(14)
+        evac_t(15)
 
         z = keep.tile([P, 8, P], F32, name="z")
         res = keep.tile([P, 8, P], F32, name="res")
@@ -326,15 +356,15 @@ def tile_gcn_pb_kernel(tc, x1, x2, adj, W3, b3, Wl, bl, out):
                 out=c3[:, ns].bitcast(FP8X4), scales=s3[:, ns], in_=gx3[:, ns, :].rearrange("p m t -> p (m t)")
             )
 
-        def logits_tile(a):
-            q = a // 2
-            if a % 2 == 0:
-                l3[q] = bank(L_BANK[q], [P, 2, P], "l3_%d" % q)
+        def logits_passes(a, chunks):
+            if chunks[0] == 0 and a in L_BANK:
+                l3[a] = bank(L_BANK[a], [P, 4, P], "l3_%d" % a)
+            a0 = min(a, 4)
             cols = slice(P * a, P * a + P)
             parts = ((cx1, sx1), (cx2, sx2), (c3, s3))
-            for c in range(3):
+            for c in chunks:
                 nc.tensor.matmul_mx(
-                    out=l3[q][:, a % 2, :],
+                    out=l3[a0][:, a - a0, :],
                     lhsT=parts[c][0][:, cols].bitcast(FP8X4),
                     lhsT_scale=parts[c][1][:, cols],
                     rhs=cw[:, c, :].bitcast(FP8X4),
@@ -343,19 +373,18 @@ def tile_gcn_pb_kernel(tc, x1, x2, adj, W3, b3, Wl, bl, out):
                     stop=(c == 2),
                 )
 
-        def logits(q):
-            for a in (2 * q, 2 * q + 1):
-                logits_tile(a)
-
-        def z_max(q):
+        def z_add(a, na):
+            a0 = min(a, 4)
             nc.vector.tensor_tensor(
-                out=z[:, 2 * q : 2 * q + 2, :],
-                in0=l3[q][:],
-                in1=consts[:, 1, :].unsqueeze(1).to_broadcast([P, 2, P]),
+                out=z[:, a : a + na, :],
+                in0=l3[a0][:, a - a0 : a - a0 + na, :],
+                in1=consts[:, 1, :].unsqueeze(1).to_broadcast([P, na, P]),
                 op=ALU.add,
             )
+
+        def z_max(a, na):
             nc.vector.tensor_reduce(
-                out=negmax[:, 2 * q : 2 * q + 2], in_=z[:, 2 * q : 2 * q + 2, :], axis=AX.X, op=ALU.max, negate=True
+                out=negmax[:, a : a + na], in_=z[:, a : a + na, :], axis=AX.X, op=ALU.max, negate=True
             )
 
         def exp_sum(a):
@@ -369,41 +398,64 @@ def tile_gcn_pb_kernel(tc, x1, x2, adj, W3, b3, Wl, bl, out):
                 accum_out=sums[:, a : a + 1],
             )
 
-        for g in range(2):
-            for tf in range(4):
-                x_pass(tf, g)
-        for a in range(4, 8):
-            xd_pass(a)
-        for tf in range(4):
-            x_evac(tf)
+        x_pass(0, 0)
+        x_pass(1, 0)
+        x_pass(2, 0)
+        x_pass(3, 0)
+        x_pass(0, 1)
+        x_pass(1, 1)
+        x_pass(2, 1)
+        x_pass(3, 1)
+        xd_pass(4)
+        xd_pass(5)
+        xd_pass(6)
+        xd_pass(7)
+        x_evac(0)
+        x_evac(1)
+        x_evac(2)
+        x_evac(3)
         x_regroup(0)
         x_regroup(1)
         quant_half(gx1, cx1, sx1, 0)
         quant_half(gx1, cx1, sx1, 1)
         xd_evac(4)
         xd_evac(5)
-        x_quant(4, 1)
-        logits_tile(4)
+        x_quant(4, 2)
+        logits_passes(4, (0, 1, 2))
+        logits_passes(5, (0, 1, 2))
+        logits_passes(0, (0, 1))
+        logits_passes(1, (0, 1))
+        logits_passes(2, (0, 1))
+        logits_passes(3, (0, 1))
         xd_evac(6)
-        x_quant(5, 1)
-        logits_tile(5)
         xd_evac(7)
-        x_quant(6, 1)
-        logits_tile(6)
-        z_max(2)
-        x_quant(7, 1)
-        logits_tile(7)
+        x_quant(6, 2)
+        logits_passes(6, (0, 1, 2))
+        logits_passes(7, (0, 1, 2))
+        z_add(4, 2)
         x_quant(0, 2)
-        logits(0)
-        z_max(3)
+        z_max(4, 2)
+        logits_passes(0, (2,))
+        logits_passes(1, (2,))
+        z_add(6, 2)
         x_quant(2, 2)
-        logits(1)
-        for a in range(4, 8):
-            exp_sum(a)
-        z_max(0)
-        z_max(1)
-        for a in range(4):
-            exp_sum(a)
+        z_max(6, 2)
+        logits_passes(2, (2,))
+        logits_passes(3, (2,))
+        exp_sum(4)
+        exp_sum(5)
+        exp_sum(6)
+        exp_sum(7)
+        z_add(0, 1)
+        z_add(1, 1)
+        z_add(2, 1)
+        z_add(3, 1)
+        z_max(0, 2)
+        z_max(2, 2)
+        exp_sum(0)
+        exp_sum(1)
+        exp_sum(2)
+        exp_sum(3)
 
         rsums = keep.tile([P, 8], F32, name="rsums")
         nc.vector.reciprocal(out=rsums[:], in_=sums[:])

@@ -59,14 +59,11 @@ def tile_gcn_pb_kernel(tc, x1, x2, adj, W3, b3, Wl, bl, out):
         adj_sb = keep.tile([P, 8, 1024], BF16, name="adj_sb")
         w3_sb = keep.tile([P, 4, 512], BF16, name="w3_sb")
         wl_sb = keep.tile([P, 12, P], BF16, name="wl_sb")
-        x2_first = x2[0 : 2 * P, :].rearrange("(m e) k -> m e k", e=2)
-        nc.sync.dma_start(out=x2_sb[:, 0, :], in_=x2_first[:, 0])
-        for u in range(2):
-            nc.sync.dma_start(
-                out=w3_sb[:, 2 * u : 2 * u + 2, :],
-                in_=W3[2 * P * u : 2 * P * (u + 1), :].rearrange("(q e) c -> q e c", e=2),
-            )
-        nc.sync.dma_start(out=x2_sb[:, 1, :], in_=x2_first[:, 1])
+        load_nodes(x2_sb, x2, 0, 1)
+        nc.sync.dma_start(
+            out=w3_sb[:].rearrange("p (u e) c -> p u e c", e=2),
+            in_=W3.rearrange("(u q e) c -> q u e c", u=2, q=P, e=2),
+        )
         load_nodes(x2_sb, x2, 1, 1)
         nc.sync.dma_start(
             out=wl_sb[:, 0:8, :].rearrange("p (cu e) n -> p cu e n", e=2),
@@ -109,19 +106,6 @@ def tile_gcn_pb_kernel(tc, x1, x2, adj, W3, b3, Wl, bl, out):
             if j == 0:
                 tps[k] = bank(k % N_T_BANKS, [P, 4, P], "tp%d" % k)
             nc.tensor.transpose(tps[k][:, j, :], t_in(k, j), ident[:])
-
-        def transpose_first(a):
-            tps[-1 - a] = bank((0, 4)[a], [P, 2, P], "tpf%d" % a)
-            for u in range(2):
-                nc.tensor.transpose(tps[-1 - a][:, u, :], t_in(0, 2 * a + u), ident[:])
-
-        def evac_first(a):
-            o = gx2[:, P * a : P * a + P, :].bitcast(F32)
-            i = tps[-1 - a][:].rearrange("p u m -> p m u")
-            if a == 0:
-                nc.vector.tensor_copy(out=o, in_=i)
-            else:
-                nc.scalar.copy(out=o, in_=i)
 
         def evac_t(k):
             if k < 4:
@@ -168,8 +152,6 @@ def tile_gcn_pb_kernel(tc, x1, x2, adj, W3, b3, Wl, bl, out):
             )
 
         def woven(i, tk):
-            if i == 0:
-                return []
             banks = range(WOVEN[i], WOVEN[i + 1])
             todo = [(k, j) for k in banks for j in range(4)]
             if len(todo) == 4:
@@ -186,13 +168,8 @@ def tile_gcn_pb_kernel(tc, x1, x2, adj, W3, b3, Wl, bl, out):
                     start=(tk == 0),
                     stop=(tk == 3),
                 )
-                if i == 0 and tk == 1:
-                    transpose_first(1)
                 for k, j in woven(i, tk):
                     transpose(k, j)
-            if i == 0:
-                for j in range(4):
-                    transpose(1, j)
 
         def evac_s(i):
             if i < 7:
@@ -223,12 +200,13 @@ def tile_gcn_pb_kernel(tc, x1, x2, adj, W3, b3, Wl, bl, out):
         wps = bank(5, [P, 512], "wps")
         for n in range(4):
             nc.tensor.matmul(out=wps[:], lhsT=warm[:, 0:P], rhs=warm[:], start=True, stop=True)
-        transpose_first(0)
-        evac_first(0)
         consts = keep.tile([P, 2, P], F32, name="consts")
+        consts = keep.tile([P, 2, P], F32, name="consts")
+        for j in range(4):
+            transpose(0, j)
+        evac_t(0)
 
         support_matmuls(0)
-        evac_first(1)
         evac_t(1)
         evac_s(0)
 
@@ -253,10 +231,10 @@ def tile_gcn_pb_kernel(tc, x1, x2, adj, W3, b3, Wl, bl, out):
 
         support_matmuls(3)
         evac_t(4)
+        quant_half(gx2, cx2, sx2, 1)
         evac_t(5)
         evac_s(3)
         nc.vector.tensor_copy(out=consts[:], in_=cps[:])
-        quant_half(gx2, cx2, sx2, 1)
 
         support_matmuls(4)
         evac_t(6)
@@ -449,9 +427,11 @@ def tile_gcn_pb_kernel(tc, x1, x2, adj, W3, b3, Wl, bl, out):
         z_add(0, 1)
         z_add(1, 1)
         z_add(2, 1)
+        z_max(0, 1)
+        z_max(1, 1)
         z_add(3, 1)
-        z_max(0, 2)
-        z_max(2, 2)
+        z_max(2, 1)
+        z_max(3, 1)
         exp_sum(0)
         exp_sum(1)
         exp_sum(2)
@@ -478,7 +458,8 @@ def tile_gcn_pb_kernel(tc, x1, x2, adj, W3, b3, Wl, bl, out):
                 op0=ALU.add,
                 op1=ALU.add,
             )
-        nc.sync.dma_start(out=out_v[:, 0:2], in_=res[:, 0:4, :].rearrange("p (s e) c -> p s e c", e=2))
+            if a in (1, 3):
+                nc.sync.dma_start(out=out_v[:, a // 2], in_=res[:, a - 1 : a + 1, :])
         for a in range(5, 8):
             nc.scalar.activation(
                 out=res[:, a, :], in_=zc[:, a - 5, :], func=ACT.Identity, bias=nlogs[:, a : a + 1], scale=1.0

@@ -198,13 +198,17 @@ def tile_gcn_pb_kernel(tc, x1, x2, adj, W3, b3, Wl, bl, out):
             )
 
         wps = bank(5, [P, 512], "wps")
-        for n in range(4):
-            nc.tensor.matmul(out=wps[:], lhsT=warm[:, 0:P], rhs=warm[:], start=True, stop=True)
-        consts = keep.tile([P, 2, P], F32, name="consts")
+
+        def warm_up(n):
+            for i in range(n):
+                nc.tensor.matmul(out=wps[:], lhsT=warm[:, 0:P], rhs=warm[:], start=True, stop=True)
+
+        warm_up(3)
         consts = keep.tile([P, 2, P], F32, name="consts")
         for j in range(4):
             transpose(0, j)
         evac_t(0)
+        warm_up(2)
 
         support_matmuls(0)
         evac_t(1)

@@ -59,11 +59,14 @@ def tile_gcn_pb_kernel(tc, x1, x2, adj, W3, b3, Wl, bl, out):
         adj_sb = keep.tile([P, 8, 1024], BF16, name="adj_sb")
         w3_sb = keep.tile([P, 4, 512], BF16, name="w3_sb")
         wl_sb = keep.tile([P, 12, P], BF16, name="wl_sb")
-        load_nodes(x2_sb, x2, 0, 1)
-        nc.sync.dma_start(
-            out=w3_sb[:].rearrange("p (u e) c -> p u e c", e=2),
-            in_=W3.rearrange("(u q e) c -> q u e c", u=2, q=P, e=2),
-        )
+        x2_first = x2[0 : 2 * P, :].rearrange("(m e) k -> m e k", e=2)
+        nc.sync.dma_start(out=x2_sb[:, 0, :], in_=x2_first[:, 0])
+        for u in range(2):
+            nc.sync.dma_start(
+                out=w3_sb[:, 2 * u : 2 * u + 2, :],
+                in_=W3[2 * P * u : 2 * P * (u + 1), :].rearrange("(q e) c -> q e c", e=2),
+            )
+        nc.sync.dma_start(out=x2_sb[:, 1, :], in_=x2_first[:, 1])
         load_nodes(x2_sb, x2, 1, 1)
         nc.sync.dma_start(
             out=wl_sb[:, 0:8, :].rearrange("p (cu e) n -> p cu e n", e=2),
@@ -106,6 +109,19 @@ def tile_gcn_pb_kernel(tc, x1, x2, adj, W3, b3, Wl, bl, out):
             if j == 0:
                 tps[k] = bank(k % N_T_BANKS, [P, 4, P], "tp%d" % k)
             nc.tensor.transpose(tps[k][:, j, :], t_in(k, j), ident[:])
+
+        def transpose_first(a):
+            tps[-1 - a] = bank((0, 4)[a], [P, 2, P], "tpf%d" % a)
+            for u in range(2):
+                nc.tensor.transpose(tps[-1 - a][:, u, :], t_in(0, 2 * a + u), ident[:])
+
+        def evac_first(a):
+            o = gx2[:, P * a : P * a + P, :].bitcast(F32)
+            i = tps[-1 - a][:].rearrange("p u m -> p m u")
+            if a == 0:
+                nc.vector.tensor_copy(out=o, in_=i)
+            else:
+                nc.scalar.copy(out=o, in_=i)
 
         def evac_t(k):
             if k < 4:
@@ -152,6 +168,8 @@ def tile_gcn_pb_kernel(tc, x1, x2, adj, W3, b3, Wl, bl, out):
             )
 
         def woven(i, tk):
+            if i == 0:
+                return []
             banks = range(WOVEN[i], WOVEN[i + 1])
             todo = [(k, j) for k in banks for j in range(4)]
             if len(todo) == 4:
@@ -168,8 +186,13 @@ def tile_gcn_pb_kernel(tc, x1, x2, adj, W3, b3, Wl, bl, out):
                     start=(tk == 0),
                     stop=(tk == 3),
                 )
+                if i == 0 and tk == 1:
+                    transpose_first(1)
                 for k, j in woven(i, tk):
                     transpose(k, j)
+            if i == 0:
+                for j in range(4):
+                    transpose(1, j)
 
         def evac_s(i):
             if i < 7:
@@ -204,13 +227,13 @@ def tile_gcn_pb_kernel(tc, x1, x2, adj, W3, b3, Wl, bl, out):
                 nc.tensor.matmul(out=wps[:], lhsT=warm[:, 0:P], rhs=warm[:], start=True, stop=True)
 
         warm_up(3)
+        transpose_first(0)
+        evac_first(0)
+        warm_up(1)
         consts = keep.tile([P, 2, P], F32, name="consts")
-        for j in range(4):
-            transpose(0, j)
-        evac_t(0)
-        warm_up(2)
 
         support_matmuls(0)
+        evac_first(1)
         evac_t(1)
         evac_s(0)
 
@@ -246,12 +269,12 @@ def tile_gcn_pb_kernel(tc, x1, x2, adj, W3, b3, Wl, bl, out):
         evac_s(4)
         regroup_s(0, 0, 512)
         quant_half(ga[0], ca[0], sa[0], 0)
-        quant_s(0, 0, 512)
 
         support_matmuls(5)
         evac_t(8)
         evac_t(9)
         evac_s(5)
+        quant_s(0, 0, 512)
         quant_half(ga[1], ca[1], sa[1], 0)
 
         support_matmuls(6)
@@ -262,11 +285,11 @@ def tile_gcn_pb_kernel(tc, x1, x2, adj, W3, b3, Wl, bl, out):
 
         support_matmuls(7)
         evac_s(7)
+        quant_half(ga[1], ca[1], sa[1], 1)
         regroup_s(1, 0, 256)
         regroup_s(1, 256, 256)
         quant_s(1, 0, 256)
         quant_s(1, 256, 256)
-        quant_half(ga[1], ca[1], sa[1], 1)
         for j in range(4):
             transpose(13, j)
         for j in range(4):

@@ -409,10 +409,10 @@ def tile_gcn_pb_kernel(tc, x1, x2, adj, W3, b3, Wl, bl, out):
         x_pass(3, 0)
         x_pass(0, 1)
         x_pass(1, 1)
-        x_pass(2, 1)
-        x_pass(3, 1)
         xd_pass(4)
         xd_pass(5)
+        x_pass(2, 1)
+        x_pass(3, 1)
         xd_pass(6)
         xd_pass(7)
         x_evac(0)
@@ -421,10 +421,10 @@ def tile_gcn_pb_kernel(tc, x1, x2, adj, W3, b3, Wl, bl, out):
         x_evac(3)
         x_regroup(0)
         x_regroup(1)
-        quant_half(gx1, cx1, sx1, 0)
         quant_half(gx1, cx1, sx1, 1)
         xd_evac(4)
         xd_evac(5)
+        quant_half(gx1, cx1, sx1, 0)
         x_quant(4, 2)
         logits_passes(4, (0, 1, 2))
         logits_passes(5, (0, 1, 2))
@@ -434,12 +434,12 @@ def tile_gcn_pb_kernel(tc, x1, x2, adj, W3, b3, Wl, bl, out):
         logits_passes(3, (0, 1))
         xd_evac(6)
         xd_evac(7)
+        z_add(4, 2)
         x_quant(6, 2)
+        z_max(4, 2)
         logits_passes(6, (0, 1, 2))
         logits_passes(7, (0, 1, 2))
-        z_add(4, 2)
         x_quant(0, 2)
-        z_max(4, 2)
         logits_passes(0, (2,))
         logits_passes(1, (2,))
         z_add(6, 2)

from contextlib import ExitStack

import concourse.mybir as mybir
from concourse.masks import make_identity

F32 = mybir.dt.float32
BF16 = mybir.dt.bfloat16
U32 = mybir.dt.uint32
U8 = mybir.dt.uint8
FP8X4 = mybir.dt.float8_e4m3fn_x4
ACT = mybir.ActivationFunctionType
ALU = mybir.AluOpType
AX = mybir.AxisListType

P = 128
FLOPS = 2 * 1024 * 512 * 512 + 2 * 1024 * 1024 * 512 + 2 * 1024 * 1536 * 128

N_T_BANKS = 5
V_EVAC = (0, 3, 5, 9)
WOVEN = (1, 2, 2, 4, 6, 8, 10, 12, 13)
X_BANK = (5, 6, 1, 7)
XD_BANK = (2, 3, 4, 0)
L_BANK = {0: 1, 1: 2, 2: 6, 3: 7, 4: 5}


def tile_gcn_pb_kernel(tc, x1, x2, adj, W3, b3, Wl, bl, out):
    nc = tc.nc
    with ExitStack() as ctx:
        keep = ctx.enter_context(tc.tile_pool(name="keep", bufs=1))
        work = ctx.enter_context(tc.tile_pool(name="work", bufs=2))
        psum = ctx.enter_context(tc.psum_pool(name="psum", bufs=1))
        ctx.enter_context(tc.manual_schedule())

        def bank(n, shape, name):
            return psum.tile(shape, F32, tag="bank%d" % n, name=name)

        def node_view(x):
            return x.rearrange("(s m e) k -> m s e k", s=4, m=P, e=2)

        def load_nodes(dst, src, s0, ns):
            nc.sync.dma_start(
                out=dst[:, 2 * s0 : 2 * (s0 + ns), :].rearrange("p (s e) k -> p s e k", e=2),
                in_=node_view(src)[:, s0 : s0 + ns],
            )

        ident = keep.tile([P, P], F32, name="ident")
        make_identity(nc, ident[:])
        warm = keep.tile([P, 512], BF16, name="warm")
        nc.vector.memset(warm[:].bitcast(U32), 0)
        zrows = keep.tile([P, P], BF16, name="zrows")
        nc.vector.memset(zrows[:], 0.0)
        ident_bf = keep.tile([P, P], BF16, name="ident_bf")
        nc.vector.tensor_copy(out=ident_bf[:], in_=ident[:])
        nc.scalar.dma_start(out=zrows[0:4, :], in_=b3.rearrange("(r c) -> r c", r=4))
        nc.scalar.dma_start(out=zrows[4:5, :], in_=bl.rearrange("(r c) -> r c", r=1))

        x2_sb = keep.tile([P, 8, 512], BF16, name="x2_sb")
        x1_sb = keep.tile([P, 8, 512], BF16, name="x1_sb")
        adj_sb = keep.tile([P, 8, 1024], BF16, name="adj_sb")
        w3_sb = keep.tile([P, 4, 512], BF16, name="w3_sb")
        wl_sb = keep.tile([P, 12, P], BF16, name="wl_sb")
        x2_first = x2[0 : 2 * P, :].rearrange("(m e) k -> m e k", e=2)
        nc.sync.dma_start(out=x2_sb[:, 0, :], in_=x2_first[:, 0])
        for u in range(2):
            nc.sync.dma_start(
                out=w3_sb[:, 2 * u : 2 * u + 2, :],
                in_=W3[2 * P * u : 2 * P * (u + 1), :].rearrange("(q e) c -> q e c", e=2),
            )
        nc.sync.dma_start(out=x2_sb[:, 1, :], in_=x2_first[:, 1])
        load_nodes(x2_sb, x2, 1, 1)
        nc.sync.dma_start(
            out=wl_sb[:, 0:8, :].rearrange("p (cu e) n -> p cu e n", e=2),
            in_=Wl[0:1024, :].rearrange("(cu q e) n -> q cu e n", cu=4, q=P, e=2),
        )
        nc.sync.dma_start(
            out=wl_sb[:, 8:12, :], in_=Wl[1024:1536, :].rearrange("(t p) n -> p t n", t=4, p=P)
        )
        load_nodes(x2_sb, x2, 2, 2)
        for s in range(4):
            load_nodes(adj_sb, adj, s, 1)
        load_nodes(x1_sb, x1, 0, 2)
        load_nodes(x1_sb, x1, 2, 2)

        x2w = x2_sb[:].bitcast(F32)
        x1w = x1_sb[:].bitcast(F32)
        adjw = adj_sb[:].bitcast(F32)

        tps = {}
        gx2 = keep.tile([P, 1024, 4], BF16, name="gx2", align_bytes=64)
        gx1 = keep.tile([P, 1024, 4], BF16, name="gx1", align_bytes=64)
        ga = [keep.tile([P, 1024, 4], BF16, name="ga%d" % g, align_bytes=64) for g in range(2)]
        cx2 = keep.tile([P, 1024], U32, name="cx2", align_bytes=64)
        sx2 = keep.tile([P, 1024], U8, name="sx2", align_bytes=64)
        cx1 = keep.tile([P, 1024], U32, name="cx1", align_bytes=64)
        sx1 = keep.tile([P, 1024], U8, name="sx1", align_bytes=64)
        ca = [keep.tile([P, 1024], U32, name="ca%d" % g, align_bytes=64) for g in range(2)]
        sa = [keep.tile([P, 1024], U8, name="sa%d" % g, align_bytes=64) for g in range(2)]

        def t_in(k, j):
            a2, u = j // 2, j % 2
            if k < 4:
                return x2w[:, 2 * k + a2, P * u : P * u + P]
            if k < 12:
                s, g = (k - 4) // 2, (k - 4) % 2
                return adjw[:, 2 * s + a2, 256 * g + P * u : 256 * g + P * u + P]
            return x1w[:, 2 * (k - 12) + a2, P * u : P * u + P]

        def transpose(k, j):
            if j == 0:
                tps[k] = bank(k % N_T_BANKS, [P, 4, P], "tp%d" % k)
            nc.tensor.transpose(tps[k][:, j, :], t_in(k, j), ident[:])

        def transpose_first(a):
            tps[-1 - a] = bank((0, 4)[a], [P, 2, P], "tpf%d" % a)
            for u in range(2):
                nc.tensor.transpose(tps[-1 - a][:, u, :], t_in(0, 2 * a + u), ident[:])

        def evac_first(a):
            o = gx2[:, P * a : P * a + P, :].bitcast(F32)
            i = tps[-1 - a][:].rearrange("p u m -> p m u")
            if a == 0:
                nc.vector.tensor_copy(out=o, in_=i)
            else:
                nc.scalar.copy(out=o, in_=i)

        def evac_t(k):
            if k < 4:
                dst, q = gx2, k
            elif k < 12:
                dst, q = ga[(k - 4) % 2], (k - 4) // 2
            else:
                dst, q = gx1, k - 12
            o = dst[:, 256 * q : 256 * q + 256, :].bitcast(F32).rearrange("p (a m) u -> p a m u", a=2)
            i = tps[k][:].rearrange("p (a u) m -> p a m u", a=2)
            if k in V_EVAC:
                nc.vector.tensor_copy(out=o, in_=i)
            else:
                nc.scalar.copy(out=o, in_=i)

        def quant_half(g, c, s, h):
            ns = slice(512 * h, 512 * h + 512)
            nc.vector.quantize_mx(
                out=c[:, ns].bitcast(FP8X4), scales=s[:, ns], in_=g[:, ns, :].rearrange("p n t -> p (n t)")
            )

        planes = [keep.tile([P, 4, 512], BF16, name="planes%d" % g) for g in range(2)]
        gs = [keep.tile([P, 512, 4], BF16, name="gs%d" % g, align_bytes=64) for g in range(2)]
        cs = [keep.tile([P, 512], U32, name="cs%d" % g, align_bytes=64) for g in range(2)]
        ss = [keep.tile([P, 512], U8, name="ss%d" % g, align_bytes=64) for g in range(2)]
        accs = {}

        def regroup(eng, dst, src):
            o = dst.rearrange("p (c i) t -> p c t i", i=4)
            i = src.rearrange("p t (c i) -> p c t i", i=4)
            if eng == "v":
                nc.vector.tensor_copy(out=o, in_=i)
            else:
                nc.scalar.copy(out=o, in_=i)

        def regroup_s(g, f0, nf):
            regroup("v", gs[g][:, f0 : f0 + nf, :], planes[g][:, :, f0 : f0 + nf])

        def quant_s(g, f0, nf):
            nc.vector.quantize_mx(
                out=cs[g][:, f0 : f0 + nf].bitcast(FP8X4),
                scales=ss[g][:, f0 : f0 + nf],
                in_=gs[g][:, f0 : f0 + nf, :].rearrange("p f t -> p (f t)"),
            )

        def woven(i, tk):
            if i == 0:
                return []
            banks = range(WOVEN[i], WOVEN[i + 1])
            todo = [(k, j) for k in banks for j in range(4)]
            if len(todo) == 4:
                return todo[2 * tk - 4 : 2 * tk - 2] if tk >= 2 else []
            return todo[2 * tk : 2 * tk + 2]

        def support_matmuls(i):
            accs[i] = bank(5 + (i if i < 3 else i + 1) % 3, [P, 512], "acc%d" % i)
            for tk in range(4):
                nc.tensor.matmul(
                    out=accs[i][:],
                    lhsT=gx2[:, P * i : P * i + P, tk],
                    rhs=w3_sb[:, tk, :],
                    start=(tk == 0),
                    stop=(tk == 3),
                )
                if i == 0 and tk == 1:
                    transpose_first(1)
                for k, j in woven(i, tk):
                    transpose(k, j)
            if i == 0:
                for j in range(4):
                    transpose(1, j)

        def evac_s(i):
            if i < 7:
                nc.scalar.copy(out=planes[i // 4][:, i % 4, :], in_=accs[i][:])
            else:
                for c in range(2):
                    nc.scalar.copy(
                        out=planes[1][:, 3, 256 * c : 256 * c + 256], in_=accs[i][:, 256 * c : 256 * c + 256]
                    )

        gw = keep.tile([P, 3, P, 4], BF16, name="gw", align_bytes=64)
        cw = keep.tile([P, 3, P], U32, name="cw", align_bytes=64)
        sw = keep.tile([P, 3, P], U8, name="sw", align_bytes=64)

        def wl_regroup(c0, nch):
            nc.vector.tensor_copy(
                out=gw[:, c0 : c0 + nch].rearrange("p c (n i) t -> p c n t i", i=4),
                in_=wl_sb[:, 4 * c0 : 4 * (c0 + nch), :].rearrange("p (c t) (n i) -> p c n t i", t=4, i=4),
            )

        def wl_quant(c0, nch):
            nc.vector.quantize_mx(
                out=cw[:, c0 : c0 + nch, :].rearrange("p c n -> p (c n)").bitcast(FP8X4),
                scales=sw[:, c0 : c0 + nch, :].rearrange("p c n -> p (c n)"),
                in_=gw[:, c0 : c0 + nch].rearrange("p c n t -> p (c n t)"),
            )

        wps = bank(5, [P, 512], "wps")

        def warm_up(n):
            for i in range(n):
                nc.tensor.matmul(out=wps[:], lhsT=warm[:, 0:P], rhs=warm[:], start=True, stop=True)

        warm_up(3)
        transpose_first(0)
        evac_first(0)
        warm_up(1)
        consts = keep.tile([P, 2, P], F32, name="consts")

        support_matmuls(0)
        evac_first(1)
        evac_t(1)
        evac_s(0)

        support_matmuls(1)
        evac_s(1)
        wl_regroup(0, 2)
        wl_regroup(2, 1)
        quant_half(gx2, cx2, sx2, 0)
        wl_quant(0, 2)
        wl_quant(2, 1)

        support_matmuls(2)
        evac_t(2)
        evac_t(3)
        evac_s(2)

        cps = bank(5, [P, 2, P], "cps")
        nc.tensor.matmul(out=cps[:, 0, :], lhsT=zrows[:], rhs=ident_bf[:], start=True, stop=True)
        nc.tensor.matmul(
            out=cps[:, 1, :], lhsT=ident_bf[:, 4:5].to_broadcast([P, P]), rhs=zrows[:], start=True, stop=True
        )

        support_matmuls(3)
        evac_t(4)
        quant_half(gx2, cx2, sx2, 1)
        evac_t(5)
        evac_s(3)
        nc.vector.tensor_copy(out=consts[:], in_=cps[:])

        support_matmuls(4)
        evac_t(6)
        evac_t(7)
        evac_s(4)
        regroup_s(0, 0, 512)
        quant_half(ga[0], ca[0], sa[0], 0)

        support_matmuls(5)
        evac_t(8)
        evac_t(9)
        evac_s(5)
        quant_s(0, 0, 512)
        quant_half(ga[1], ca[1], sa[1], 0)

        support_matmuls(6)
        evac_t(10)
        evac_t(11)
        evac_s(6)
        quant_half(ga[0], ca[0], sa[0], 1)

        support_matmuls(7)
        evac_s(7)
        quant_half(ga[1], ca[1], sa[1], 1)
        regroup_s(1, 0, 256)
        regroup_s(1, 256, 256)
        quant_s(1, 0, 256)
        quant_s(1, 256, 256)
        for j in range(4):
            transpose(13, j)
        for j in range(4):
            transpose(14, j)
        for j in range(4):
            transpose(15, j)
        evac_t(12)
        evac_t(13)
        evac_t(14)
        evac_t(15)

        z = keep.tile([P, 8, P], F32, name="z")
        res = keep.tile([P, 8, P], F32, name="res")
        negmax = keep.tile([P, 8], F32, name="negmax")
        sums = keep.tile([P, 8], F32, name="sums")
        pl3 = keep.tile([P, 4, 512], BF16, name="pl3")
        gx3 = keep.tile([P, 1024, 4], BF16, name="gx3", align_bytes=64)
        c3 = keep.tile([P, 1024], U32, name="c3", align_bytes=64)
        s3 = keep.tile([P, 1024], U8, name="s3", align_bytes=64)
        x3ps = {}
        l3 = {}

        def x_mm(ps, g, tf, ns):
            fs = slice(P * tf, P * tf + P)
            nc.tensor.matmul_mx(
                out=ps,
                lhsT=cs[g][:, fs].bitcast(FP8X4),
                lhsT_scale=ss[g][:, fs],
                rhs=ca[g][:, ns].bitcast(FP8X4),
                rhs_scale=sa[g][:, ns],
                start=(g == 0),
                stop=(g == 1),
            )

        def x_pass(tf, g):
            if g == 0:
                x3ps[tf] = bank(X_BANK[tf], [P, 512], "x3ps%d" % tf)
            x_mm(x3ps[tf][:], g, tf, slice(0, 512))

        def x_evac(tf):
            nc.scalar.activation(
                out=pl3[:, tf, :],
                in_=x3ps[tf][:],
                func=ACT.Identity,
                bias=consts[:, 0, tf : tf + 1],
                scale=1.0,
            )

        def x_regroup(q):
            regroup("s", gx3[:, 256 * q : 256 * q + 256, :], pl3[:, :, 256 * q : 256 * q + 256])

        def xd_pass(a):
            x3ps[a] = bank(XD_BANK[a - 4], [P, 4, P], "x3ps%d" % a)
            for tf in range(4):
                for g in range(2):
                    x_mm(x3ps[a][:, tf, :], g, tf, slice(P * a, P * a + P))

        def xd_evac(a):
            nc.vector.tensor_tensor(
                out=gx3[:, P * a : P * a + P, :],
                in0=x3ps[a][:].rearrange("p t m -> p m t"),
                in1=consts[:, 0, 0:4].unsqueeze(1).to_broadcast([P, P, 4]),
                op=ALU.add,
            )

        def x_quant(a, na):
            ns = slice(P * a, P * (a + na))
            nc.vector.quantize_mx(
                out=c3[:, ns].bitcast(FP8X4), scales=s3[:, ns], in_=gx3[:, ns, :].rearrange("p m t -> p (m t)")
            )

        def logits_passes(a, chunks):
            if chunks[0] == 0 and a in L_BANK:
                l3[a] = bank(L_BANK[a], [P, 4, P], "l3_%d" % a)
            a0 = min(a, 4)
            cols = slice(P * a, P * a + P)
            parts = ((cx1, sx1), (cx2, sx2), (c3, s3))
            for c in chunks:
                nc.tensor.matmul_mx(
                    out=l3[a0][:, a - a0, :],
                    lhsT=parts[c][0][:, cols].bitcast(FP8X4),
                    lhsT_scale=parts[c][1][:, cols],
                    rhs=cw[:, c, :].bitcast(FP8X4),
                    rhs_scale=sw[:, c, :],
                    start=(c == 0),
                    stop=(c == 2),
                )

        def z_add(a, na):
            a0 = min(a, 4)
            nc.vector.tensor_tensor(
                out=z[:, a : a + na, :],
                in0=l3[a0][:, a - a0 : a - a0 + na, :],
                in1=consts[:, 1, :].unsqueeze(1).to_broadcast([P, na, P]),
                op=ALU.add,
            )

        def z_max(a, na):
            nc.vector.tensor_reduce(
                out=negmax[:, a : a + na], in_=z[:, a : a + na, :], axis=AX.X, op=ALU.max, negate=True
            )

        def exp_sum(a):
            junk = work.tile([P, P], BF16, tag="junk", name="junk%d" % a)
            nc.scalar.activation(
                out=junk[:],
                in_=z[:, a, :],
                func=ACT.Exp,
                bias=negmax[:, a : a + 1],
                scale=1.0,
                accum_out=sums[:, a : a + 1],
            )

        x_pass(0, 0)
        x_pass(1, 0)
        x_pass(2, 0)
        x_pass(3, 0)
        x_pass(0, 1)
        x_pass(1, 1)
        xd_pass(4)
        xd_pass(5)
        x_pass(2, 1)
        x_pass(3, 1)
        xd_pass(6)
        xd_pass(7)
        x_evac(0)
        x_evac(1)
        x_evac(2)
        x_evac(3)
        x_regroup(0)
        x_regroup(1)
        quant_half(gx1, cx1, sx1, 1)
        xd_evac(4)
        xd_evac(5)
        quant_half(gx1, cx1, sx1, 0)
        x_quant(4, 2)
        logits_passes(4, (0, 1, 2))
        logits_passes(5, (0, 1, 2))
        logits_passes(0, (0, 1))
        logits_passes(1, (0, 1))
        logits_passes(2, (0, 1))
        logits_passes(3, (0, 1))
        xd_evac(6)
        xd_evac(7)
        z_add(4, 2)
        x_quant(6, 2)
        z_max(4, 2)
        logits_passes(6, (0, 1, 2))
        logits_passes(7, (0, 1, 2))
        x_quant(0, 2)
        logits_passes(0, (2,))
        logits_passes(1, (2,))
        z_add(6, 2)
        x_quant(2, 2)
        z_max(6, 2)
        logits_passes(2, (2,))
        logits_passes(3, (2,))
        exp_sum(4)
        exp_sum(5)
        exp_sum(6)
        exp_sum(7)
        z_add(0, 1)
        z_add(1, 1)
        z_add(2, 1)
        z_max(0, 1)
        z_max(1, 1)
        z_add(3, 1)
        z_max(2, 1)
        z_max(3, 1)
        exp_sum(0)
        exp_sum(1)
        exp_sum(2)
        exp_sum(3)

        rsums = keep.tile([P, 8], F32, name="rsums")
        nc.vector.reciprocal(out=rsums[:], in_=sums[:])
        zc = keep.tile([P, 3, P], F32, name="zc")
        nc.vector.tensor_tensor(
            out=zc[:],
            in0=z[:, 5:8, :],
            in1=negmax[:, 5:8].unsqueeze(2).to_broadcast([P, 3, P]),
            op=ALU.add,
        )
        nlogs = keep.tile([P, 8], F32, name="nlogs")
        nc.scalar.activation(out=nlogs[:], in_=rsums[:], func=ACT.Ln)
        out_v = out.rearrange("(s m e) c -> m s e c", s=4, m=P, e=2)
        for a in range(5):
            nc.vector.tensor_scalar(
                out=res[:, a, :],
                in0=z[:, a, :],
                scalar1=negmax[:, a : a + 1],
                scalar2=nlogs[:, a : a + 1],
                op0=ALU.add,
                op1=ALU.add,
            )
            if a in (1, 3):
                nc.sync.dma_start(out=out_v[:, a // 2], in_=res[:, a - 1 : a + 1, :])
        for a in range(5, 8):
            nc.scalar.activation(
                out=res[:, a, :], in_=zc[:, a - 5, :], func=ACT.Identity, bias=nlogs[:, a : a + 1], scale=1.0
            )
        nc.sync.dma_start(out=out_v[:, 2:4], in_=res[:, 4:8, :].rearrange("p (s e) c -> p s e c", e=2))
